import numpy as np
import ml_dtypes


def mxq(x, axis, fmt="e4m3"):
    dtype, down = {"e4m3": (ml_dtypes.float8_e4m3fn, 7), "e5m2": (ml_dtypes.float8_e5m2, 14)}[fmt]
    v = np.moveaxis(np.asarray(x, np.float32).astype(ml_dtypes.bfloat16).astype(np.float64), axis, -1)
    blocks = v.reshape(v.shape[:-1] + (-1, 32))
    amax = np.abs(blocks).max(-1, keepdims=True)
    byte = np.maximum(np.where(amax > 0, np.frexp(amax)[1] - 1 + 127, 0) - down, 1)
    scale = np.exp2(byte - 127.0)
    codes = (blocks / scale).astype(np.float32).astype(dtype).astype(np.float64)
    return np.moveaxis((codes * scale).reshape(v.shape), -1, axis)


BF16 = ml_dtypes.bfloat16


def bf(x):
    return np.asarray(x, np.float32).astype(BF16)


def f64(x):
    return np.asarray(x).astype(np.float64)


B, C, H, W, G = 2, 512, 32, 32, 8
N = H * W
THRESHOLD = 16.0


def draw_x():
    q = np.linalg.qr(np.random.standard_normal((C, C)))[0]
    ia = np.random.randint(0, G, (B, N))
    ib = np.random.randint(0, G, (B, N)) + G
    codes = 0.55 * THRESHOLD * (q[:, ia] + q[:, ib]).transpose(1, 0, 2)
    noise = 0.212 * THRESHOLD / np.sqrt(C) * np.random.standard_normal((B, C, N))
    return (codes + noise).reshape(B, C, H, W)


def setup_inputs():
    return {"x": bf(draw_x()),
            "W_fc": bf(np.random.standard_normal((C, C)) * 2.0 / np.sqrt(C)),
            "b_fc": bf(np.random.standard_normal(C) * 0.2)}


def reference(x, W_fc, b_fc):
    xf = f64(x).reshape(B, C, N).transpose(0, 2, 1)
    sq = (xf * xf).sum(-1)
    d2 = sq[:, :, None] + sq[:, None, :] - 2.0 * (xf @ xf.transpose(0, 2, 1))
    dist = np.sqrt(np.maximum(d2, 0.0))
    inc = np.where(dist < THRESHOLD, 1.0, 0.0)
    incq = mxq(inc, 2, "e4m3")
    xe = xf @ f64(W_fc).T + f64(b_fc)
    deg_e = inc.sum(1)
    edge = incq @ mxq(xe, 1, "e4m3")
    edge = np.where(deg_e > 0, 1.0 / deg_e, 0.0)[:, :, None] * edge
    deg_v = inc.sum(2)
    vert = incq @ mxq(edge, 1, "e4m3")
    vert = np.where(deg_v > 0, 1.0 / deg_v, 0.0)[:, :, None] * vert
    out = vert + xf
    return out.transpose(0, 2, 1).reshape(B, C, H, W)

@@ -1,0 +1,367 @@
+from contextlib import ExitStack
+
+import concourse.mybir as mybir
+from concourse.masks import make_identity
+
+F32 = mybir.dt.float32
+BF16 = mybir.dt.bfloat16
+U32 = mybir.dt.uint32
+U8 = mybir.dt.uint8
+FP8X4 = mybir.dt.float8_e4m3fn_x4
+ALU = mybir.AluOpType
+ACT = mybir.ActivationFunctionType
+AXIS = mybir.AxisListType
+
+BATCH = 2
+CHANNELS = 512
+PIXELS = 1024
+THRESHOLD = 16.0
+
+P = 128
+PACK = 4
+K_PASS = P * PACK
+BANK = 512
+
+CHUNKS = CHANNELS // P
+BLOCKS = PIXELS // P
+PASSES = PIXELS // K_PASS
+HALVES = PIXELS // BANK
+
+INC_WAITING = 5
+
+FLOPS = BATCH * (2 * PIXELS * PIXELS * CHANNELS * 3 + 2 * PIXELS * CHANNELS * CHANNELS)
+
+
+def block(index):
+    return slice(index * P, (index + 1) * P)
+
+
+def half(index):
+    return slice(index * BANK, (index + 1) * BANK)
+
+
+def tile_hypercomputemodule_pa_kernel(tc, x, W_fc, b_fc, out):
+    nc = tc.nc
+    x_dram = x.rearrange("b (cc p) h w -> b p cc (h w)", p=P)
+    out_dram = out.rearrange("b (ob p) h w -> b p ob (h w)", p=P)
+
+    with ExitStack() as ctx:
+        const = ctx.enter_context(tc.tile_pool(name="const", bufs=1))
+        keep = ctx.enter_context(tc.tile_pool(name="keep", bufs=1))
+        stage = ctx.enter_context(tc.tile_pool(name="stage", bufs=2))
+        results = ctx.enter_context(tc.tile_pool(name="results", bufs=8))
+        psum = ctx.enter_context(tc.psum_pool(name="psum", bufs=8))
+        ctx.enter_context(tc.manual_schedule())
+
+        batches = range(BATCH)
+        x_sb = [keep.tile([P, CHUNKS, PIXELS], BF16, name="x_sb%d" % b) for b in batches]
+        diag_sb = [keep.tile([P, BLOCKS, P], F32, name="diag_sb%d" % b) for b in batches]
+        h_col = [keep.tile([P, BLOCKS], F32, name="h_col%d" % b) for b in batches]
+        h_row = [keep.tile([P, PIXELS], F32, name="h_row%d" % b) for b in batches]
+        r_col = [keep.tile([P, BLOCKS], F32, name="r_col%d" % b) for b in batches]
+        r_row = [keep.tile([P, PIXELS], F32, name="r_row%d" % b) for b in batches]
+        inc = [keep.tile([P, BLOCKS, PIXELS], BF16, name="inc%d" % b) for b in batches]
+        deg_upper = [keep.tile([P, BLOCKS, 1 + HALVES], F32, name="deg_upper%d" % b) for b in batches]
+        deg_lower = [keep.tile([P, BLOCKS, 1 + HALVES], F32, name="deg_lower%d" % b) for b in batches]
+        inc_codes = [
+            keep.tile([P, PASSES, PIXELS], U32, name="inc_codes%d" % b, align_bytes=64) for b in batches
+        ]
+        inc_scales = [
+            keep.tile([P, PASSES, PIXELS], U8, name="inc_scales%d" % b, align_bytes=64) for b in batches
+        ]
+        xe_codes = [
+            keep.tile([P, PASSES, CHANNELS], U32, name="xe_codes%d" % b, align_bytes=64) for b in batches
+        ]
+        xe_scales = [
+            keep.tile([P, PASSES, CHANNELS], U8, name="xe_scales%d" % b, align_bytes=64) for b in batches
+        ]
+        edge_codes = [
+            keep.tile([P, PASSES, CHANNELS], U32, name="edge_codes%d" % b, align_bytes=64) for b in batches
+        ]
+        edge_scales = [
+            keep.tile([P, PASSES, CHANNELS], U8, name="edge_scales%d" % b, align_bytes=64) for b in batches
+        ]
+        waiting = {}
+
+        w_sb = const.tile([P, CHUNKS, CHANNELS], BF16)
+        w_t = const.tile([P, CHUNKS, CHANNELS], BF16)
+        for cc in range(CHUNKS):
+            nc.sync.dma_start(out=x_sb[0][:, cc, :], in_=x_dram[0, :, cc, :])
+        nc.sync.dma_start(out=w_sb[:], in_=W_fc.rearrange("(ob p) c -> p ob c", p=P))
+        for cc in range(CHUNKS):
+            nc.sync.dma_start(out=x_sb[1][:, cc, :], in_=x_dram[1, :, cc, :])
+        bias_row = const.tile([P, CHANNELS], BF16)
+        nc.scalar.dma_start(out=bias_row[:], in_=b_fc.partition_broadcast(P))
+
+        ident_bf = const.tile([P, P], BF16)
+        make_identity(nc, ident_bf[:])
+        ident_f32 = const.tile([P, P], F32)
+        make_identity(nc, ident_f32[:])
+        for b in batches:
+            nc.vector.memset(deg_upper[b][:], 0.0)
+            nc.vector.memset(deg_lower[b][:], 0.0)
+
+        def gram_diagonal(b, g):
+            bank = psum.tile([P, PACK, P], F32, tag="bank")
+            for t in range(PACK):
+                rows = block(PACK * g + t)
+                for cc in range(CHUNKS):
+                    nc.tensor.matmul(
+                        out=bank[:, t, :],
+                        lhsT=x_sb[b][:, cc, rows],
+                        rhs=x_sb[b][:, cc, rows],
+                        start=(cc == 0),
+                        stop=(cc == CHUNKS - 1),
+                    )
+            nc.scalar.copy(out=diag_sb[b][:, PACK * g : PACK * (g + 1), :], in_=bank[:])
+
+        def transpose_weights():
+            for cc in range(CHUNKS):
+                bank = psum.tile([P, CHANNELS], BF16, tag="bank")
+                for ob in range(CHUNKS):
+                    nc.tensor.transpose(bank[:, block(ob)], w_sb[:, ob, block(cc)], ident_bf[:])
+                nc.vector.tensor_copy(out=w_t[:, cc, :], in_=bank[:])
+
+        def half_norms(b):
+            masked = stage.tile([P, BLOCKS, P], F32)
+            nc.gpsimd.tensor_tensor(
+                out=masked[:],
+                in0=diag_sb[b][:],
+                in1=ident_f32[:].unsqueeze(1).to_broadcast([P, BLOCKS, P]),
+                op=ALU.mult,
+            )
+            sq = stage.tile([P, BLOCKS], F32)
+            nc.vector.tensor_reduce(out=sq[:], in_=masked[:], axis=AXIS.X, op=ALU.add)
+            nc.vector.tensor_scalar(
+                out=h_col[b][:],
+                in0=sq[:],
+                scalar1=0.5,
+                scalar2=-THRESHOLD * THRESHOLD / 4.0,
+                op0=ALU.mult,
+                op1=ALU.add,
+            )
+
+        def spread(col, row):
+            for g in range(HALVES):
+                bank = psum.tile([P, PACK, P], F32, tag="bank")
+                for t in range(PACK):
+                    r = PACK * g + t
+                    nc.tensor.transpose(bank[:, t, :], col[:, r : r + 1].to_broadcast([P, P]), ident_f32[:])
+                nc.scalar.copy(out=row[:, half(g)], in_=bank[:].rearrange("p t n -> p (t n)"))
+
+        def compare(b, r, gram, cols, piece):
+            nc.vector.scalar_tensor_tensor(
+                out=inc[b][:, r, cols],
+                in0=gram,
+                scalar=h_col[b][:, r : r + 1],
+                in1=h_row[b][:, cols],
+                op0=ALU.subtract,
+                op1=ALU.is_gt,
+                accum_out=deg_upper[b][:, r, piece : piece + 1],
+            )
+
+        def upper(b, r, hf):
+            first = max(hf * BANK, (r + 1) * P)
+            width = (hf + 1) * BANK - first
+            cols = slice(first, first + width)
+            bank = psum.tile([P, BANK], F32, tag="bank")
+            for cc in range(CHUNKS):
+                nc.tensor.matmul(
+                    out=bank[:, :width],
+                    lhsT=x_sb[b][:, cc, block(r)],
+                    rhs=x_sb[b][:, cc, cols],
+                    start=(cc == 0),
+                    stop=(cc == CHUNKS - 1),
+                )
+            compare(b, r, bank[:, :width], cols, 1 + hf)
+
+        def lower(b, r, hf):
+            first = hf * PACK
+            last = min(r, first + PACK)
+            bank = psum.tile([P, BANK], BF16, tag="bank")
+            for q in range(first, last):
+                nc.tensor.transpose(bank[:, block(q - first)], inc[b][:, q, block(r)], ident_bf[:])
+            nc.scalar.activation(
+                out=inc[b][:, r, first * P : last * P],
+                in_=bank[:, : (last - first) * P],
+                func=ACT.Copy,
+                accum_out=deg_lower[b][:, r, 1 + hf : 2 + hf],
+            )
+
+        def reciprocal_degrees(b):
+            both = stage.tile([P, BLOCKS, 1 + HALVES], F32)
+            nc.vector.tensor_tensor(out=both[:], in0=deg_upper[b][:], in1=deg_lower[b][:], op=ALU.add)
+            degree = stage.tile([P, BLOCKS], F32)
+            nc.vector.tensor_reduce(out=degree[:], in_=both[:], axis=AXIS.X, op=ALU.add)
+            at_least_one = stage.tile([P, BLOCKS], F32)
+            nc.vector.tensor_scalar_max(out=at_least_one[:], in0=degree[:], scalar1=1.0)
+            nc.vector.reciprocal(out=r_col[b][:], in_=at_least_one[:])
+
+        def regroup(engine_copy, grouped, rows):
+            engine_copy(
+                out=grouped.rearrange("p (c i) t -> p c t i", i=4),
+                in_=rows.rearrange("p t (c i) -> p c t i", i=4),
+            )
+
+        def gpsimd_copy(out, in_):
+            nc.gpsimd.tensor_scalar(out=out, in0=in_, scalar1=1.0, scalar2=0.0, op0=ALU.mult, op1=ALU.add)
+
+        def regroup_incidence(engine_copy, b, g, hf):
+            inc_grouped = stage.tile([P, BANK, PACK], BF16, align_bytes=64, bufs=INC_WAITING)
+            regroup(engine_copy, inc_grouped[:], inc[b][:, PACK * g : PACK * (g + 1), half(hf)])
+            waiting[(b, g, hf)] = inc_grouped
+
+        def quantise_incidence(b, g, hf):
+            nc.vector.quantize_mx(
+                out=inc_codes[b][:, g, half(hf)].bitcast(FP8X4),
+                scales=inc_scales[b][:, g, half(hf)],
+                in_=waiting[(b, g, hf)][:].rearrange("p c t -> p (c t)"),
+            )
+
+        def project(b, g):
+            xe_grouped = stage.tile([P, CHANNELS, PACK], BF16, align_bytes=64)
+            for ob in range(CHUNKS):
+                bank = psum.tile([P, PACK, P], F32, tag="bank")
+                for t in range(PACK):
+                    for cc in range(CHUNKS):
+                        nc.tensor.matmul(
+                            out=bank[:, t, :],
+                            lhsT=x_sb[b][:, cc, block(PACK * g + t)],
+                            rhs=w_t[:, cc, block(ob)],
+                            start=(cc == 0),
+                            stop=(cc == CHUNKS - 1),
+                        )
+                nc.vector.tensor_tensor(
+                    out=xe_grouped[:, block(ob), :],
+                    in0=bank[:].rearrange("p t o -> p o t"),
+                    in1=bias_row[:, block(ob)].unsqueeze(2).to_broadcast([P, P, PACK]),
+                    op=ALU.add,
+                )
+            nc.vector.quantize_mx(
+                out=xe_codes[b][:, g, :].bitcast(FP8X4),
+                scales=xe_scales[b][:, g, :],
+                in_=xe_grouped[:].rearrange("p o t -> p (o t)"),
+            )
+
+        def edges(b, g_out):
+            edge_rows = stage.tile([P, PACK, CHANNELS], BF16)
+            for t in range(PACK):
+                r = PACK * g_out + t
+                bank = psum.tile([P, CHANNELS], F32, tag="bank")
+                for g in range(PASSES):
+                    nc.tensor.matmul_mx(
+                        out=bank[:],
+                        lhsT=inc_codes[b][:, g, block(r)].bitcast(FP8X4),
+                        lhsT_scale=inc_scales[b][:, g, block(r)],
+                        rhs=xe_codes[b][:, g, :].bitcast(FP8X4),
+                        rhs_scale=xe_scales[b][:, g, :],
+                        start=(g == 0),
+                        stop=(g == PASSES - 1),
+                    )
+                nc.scalar.activation(
+                    out=edge_rows[:, t, :], in_=bank[:], func=ACT.Copy, scale=r_col[b][:, r : r + 1]
+                )
+            edge_grouped = stage.tile([P, CHANNELS, PACK], BF16, align_bytes=64)
+            regroup(nc.vector.tensor_copy, edge_grouped[:], edge_rows[:])
+            nc.vector.quantize_mx(
+                out=edge_codes[b][:, g_out, :].bitcast(FP8X4),
+                scales=edge_scales[b][:, g_out, :],
+                in_=edge_grouped[:].rearrange("p o t -> p (o t)"),
+            )
+
+        def vertices(b, ob):
+            for hf in range(HALVES):
+                bank = psum.tile([P, BANK], F32, tag="bank")
+                for g in range(PASSES):
+                    nc.tensor.matmul_mx(
+                        out=bank[:],
+                        lhsT=edge_codes[b][:, g, block(ob)].bitcast(FP8X4),
+                        lhsT_scale=edge_scales[b][:, g, block(ob)],
+                        rhs=inc_codes[b][:, g, half(hf)].bitcast(FP8X4),
+                        rhs_scale=inc_scales[b][:, g, half(hf)],
+                        start=(g == 0),
+                        stop=(g == PASSES - 1),
+                    )
+                vert = results.tile([P, BANK], F32)
+                nc.vector.tensor_tensor(out=vert[:], in0=bank[:], in1=r_row[b][:, half(hf)], op=ALU.mult)
+                result = results.tile([P, BANK], F32)
+                adder = nc.vector if (ob * HALVES + hf) % 3 == 2 else nc.gpsimd
+                adder.tensor_tensor(out=result[:], in0=vert[:], in1=x_sb[b][:, ob, half(hf)], op=ALU.add)
+                nc.sync.dma_start(out=out_dram[b, :, ob, half(hf)], in_=result[:])
+
+        def compare_diagonal(b):
+            for r in range(BLOCKS):
+                compare(b, r, diag_sb[b][:, r, :], block(r), 0)
+
+        def square(b):
+            for r in range(PACK):
+                upper(b, r, 1)
+
+        def triangles(b):
+            for r in range(BLOCKS):
+                if r % PACK < PACK - 1:
+                    upper(b, r, r // PACK)
+
+        def mirror_square(b):
+            for r in range(PACK, BLOCKS):
+                lower(b, r, 0)
+
+        def mirror_triangles(b):
+            for r in range(BLOCKS):
+                if r % PACK > 0:
+                    lower(b, r, r // PACK)
+
+
+        gram_diagonal(0, 0)
+        transpose_weights()
+        gram_diagonal(0, 1)
+        project(0, 0)
+        half_norms(0)
+        gram_diagonal(1, 0)
+        gram_diagonal(1, 1)
+        project(0, 1)
+        half_norms(1)
+        spread(h_col[0], h_row[0])
+
+        compare_diagonal(0)
+        square(0)
+        regroup_incidence(gpsimd_copy, 0, 0, 1)
+        triangles(0)
+        spread(h_col[1], h_row[1])
+        mirror_square(0)
+        mirror_triangles(0)
+        quantise_incidence(0, 0, 1)
+        regroup_incidence(nc.scalar.copy, 0, 1, 0)
+        regroup_incidence(nc.scalar.copy, 0, 0, 0)
+        regroup_incidence(gpsimd_copy, 0, 1, 1)
+
+        compare_diagonal(1)
+        square(1)
+        regroup_incidence(gpsimd_copy, 1, 0, 1)
+        quantise_incidence(0, 1, 0)
+        quantise_incidence(0, 1, 1)
+        triangles(1)
+        quantise_incidence(0, 0, 0)
+        reciprocal_degrees(0)
+        mirror_square(1)
+        mirror_triangles(1)
+        quantise_incidence(1, 0, 1)
+        regroup_incidence(nc.scalar.copy, 1, 1, 0)
+        regroup_incidence(nc.scalar.copy, 1, 0, 0)
+        regroup_incidence(gpsimd_copy, 1, 1, 1)
+
+        project(1, 0)
+        quantise_incidence(1, 1, 0)
+        quantise_incidence(1, 1, 1)
+        reciprocal_degrees(1)
+        project(1, 1)
+        quantise_incidence(1, 0, 0)
+        spread(r_col[0], r_row[0])
+        spread(r_col[1], r_row[1])
+
+        for b in batches:
+            for g_out in range(PASSES):
+                edges(b, g_out)
+        for b in batches:
+            for ob in range(CHUNKS):
+                vertices(b, ob)

@@ -59,7 +59,6 @@ def tile_hypercomputemodule_pa_kernel(tc, x, W_fc, b_fc, out):
         h_col = [keep.tile([P, BLOCKS], F32, name="h_col%d" % b) for b in batches]
         h_row = [keep.tile([P, PIXELS], F32, name="h_row%d" % b) for b in batches]
         r_col = [keep.tile([P, BLOCKS], F32, name="r_col%d" % b) for b in batches]
-        r_row = [keep.tile([P, PIXELS], F32, name="r_row%d" % b) for b in batches]
         inc = [keep.tile([P, BLOCKS, PIXELS], BF16, name="inc%d" % b) for b in batches]
         deg_upper = [keep.tile([P, BLOCKS, 1 + HALVES], F32, name="deg_upper%d" % b) for b in batches]
         deg_lower = [keep.tile([P, BLOCKS, 1 + HALVES], F32, name="deg_lower%d" % b) for b in batches]
@@ -85,11 +84,11 @@ def tile_hypercomputemodule_pa_kernel(tc, x, W_fc, b_fc, out):
 
         w_sb = const.tile([P, CHUNKS, CHANNELS], BF16)
         w_t = const.tile([P, CHUNKS, CHANNELS], BF16)
-        for cc in range(CHUNKS):
-            nc.sync.dma_start(out=x_sb[0][:, cc, :], in_=x_dram[0, :, cc, :])
+        nc.sync.dma_start(out=x_sb[0][:, :, half(0)], in_=x_dram[0, :, :, half(0)])
         nc.sync.dma_start(out=w_sb[:], in_=W_fc.rearrange("(ob p) c -> p ob c", p=P))
-        for cc in range(CHUNKS):
-            nc.sync.dma_start(out=x_sb[1][:, cc, :], in_=x_dram[1, :, cc, :])
+        nc.sync.dma_start(out=x_sb[0][:, :, half(1)], in_=x_dram[0, :, :, half(1)])
+        for hf in range(HALVES):
+            nc.sync.dma_start(out=x_sb[1][:, :, half(hf)], in_=x_dram[1, :, :, half(hf)])
         bias_row = const.tile([P, CHANNELS], BF16)
         nc.scalar.dma_start(out=bias_row[:], in_=b_fc.partition_broadcast(P))
 
@@ -269,24 +268,37 @@ def tile_hypercomputemodule_pa_kernel(tc, x, W_fc, b_fc, out):
                 in_=edge_grouped[:].rearrange("p o t -> p (o t)"),
             )
 
-        def vertices(b, ob):
-            for hf in range(HALVES):
-                bank = psum.tile([P, BANK], F32, tag="bank")
+        def vertices(b, hf):
+            vert = stage.tile([P, PACK, CHANNELS], F32)
+            for t in range(PACK):
+                r = PACK * hf + t
+                bank = psum.tile([P, CHANNELS], F32, tag="bank")
                 for g in range(PASSES):
                     nc.tensor.matmul_mx(
                         out=bank[:],
-                        lhsT=edge_codes[b][:, g, block(ob)].bitcast(FP8X4),
-                        lhsT_scale=edge_scales[b][:, g, block(ob)],
-                        rhs=inc_codes[b][:, g, half(hf)].bitcast(FP8X4),
-                        rhs_scale=inc_scales[b][:, g, half(hf)],
+                        lhsT=inc_codes[b][:, g, block(r)].bitcast(FP8X4),
+                        lhsT_scale=inc_scales[b][:, g, block(r)],
+                        rhs=edge_codes[b][:, g, :].bitcast(FP8X4),
+                        rhs_scale=edge_scales[b][:, g, :],
                         start=(g == 0),
                         stop=(g == PASSES - 1),
                     )
-                vert = results.tile([P, BANK], F32)
-                nc.vector.tensor_tensor(out=vert[:], in0=bank[:], in1=r_row[b][:, half(hf)], op=ALU.mult)
+                nc.scalar.activation(out=vert[:, t, :], in_=bank[:], func=ACT.Copy, scale=r_col[b][:, r : r + 1])
+            waiting[(b, hf)] = vert
+
+        def finish(b, hf):
+            vert = waiting[(b, hf)]
+            for ob in range(CHUNKS):
+                bank = psum.tile([P, PACK, P], F32, tag="bank")
+                for t in range(PACK):
+                    nc.tensor.transpose(bank[:, t, :], vert[:, t, block(ob)], ident_f32[:])
                 result = results.tile([P, BANK], F32)
-                adder = nc.vector if (ob * HALVES + hf) % 3 == 2 else nc.gpsimd
-                adder.tensor_tensor(out=result[:], in0=vert[:], in1=x_sb[b][:, ob, half(hf)], op=ALU.add)
+                nc.vector.tensor_tensor(
+                    out=result[:],
+                    in0=bank[:].rearrange("p t i -> p (t i)"),
+                    in1=x_sb[b][:, ob, half(hf)],
+                    op=ALU.add,
+                )
                 nc.sync.dma_start(out=out_dram[b, :, ob, half(hf)], in_=result[:])
 
         def compare_diagonal(b):
@@ -314,11 +326,11 @@ def tile_hypercomputemodule_pa_kernel(tc, x, W_fc, b_fc, out):
 
         gram_diagonal(0, 0)
         transpose_weights()
-        gram_diagonal(0, 1)
         project(0, 0)
-        half_norms(0)
+        gram_diagonal(0, 1)
         gram_diagonal(1, 0)
         gram_diagonal(1, 1)
+        half_norms(0)
         project(0, 1)
         half_norms(1)
         spread(h_col[0], h_row[0])
@@ -356,12 +368,15 @@ def tile_hypercomputemodule_pa_kernel(tc, x, W_fc, b_fc, out):
         reciprocal_degrees(1)
         project(1, 1)
         quantise_incidence(1, 0, 0)
-        spread(r_col[0], r_row[0])
-        spread(r_col[1], r_row[1])
 
         for b in batches:
             for g_out in range(PASSES):
                 edges(b, g_out)
-        for b in batches:
-            for ob in range(CHUNKS):
-                vertices(b, ob)
+        vertices(0, 0)
+        vertices(0, 1)
+        finish(0, 0)
+        vertices(1, 0)
+        finish(0, 1)
+        vertices(1, 1)
+        finish(1, 0)
+        finish(1, 1)

@@ -27,7 +27,7 @@ BLOCKS = PIXELS // P
 PASSES = PIXELS // K_PASS
 HALVES = PIXELS // BANK
 
-INC_WAITING = 5
+INC_WAITING = 6
 
 FLOPS = BATCH * (2 * PIXELS * PIXELS * CHANNELS * 3 + 2 * PIXELS * CHANNELS * CHANNELS)
 
@@ -61,7 +61,7 @@ def tile_hypercomputemodule_pa_kernel(tc, x, W_fc, b_fc, out):
         r_col = [keep.tile([P, BLOCKS], F32, name="r_col%d" % b) for b in batches]
         inc = [keep.tile([P, BLOCKS, PIXELS], BF16, name="inc%d" % b) for b in batches]
         deg_upper = [keep.tile([P, BLOCKS, 1 + HALVES], F32, name="deg_upper%d" % b) for b in batches]
-        deg_lower = [keep.tile([P, BLOCKS, 1 + HALVES], F32, name="deg_lower%d" % b) for b in batches]
+        deg_lower = [keep.tile([P, BLOCKS], F32, name="deg_lower%d" % b) for b in batches]
         inc_codes = [
             keep.tile([P, PASSES, PIXELS], U32, name="inc_codes%d" % b, align_bytes=64) for b in batches
         ]
@@ -81,7 +81,14 @@ def tile_hypercomputemodule_pa_kernel(tc, x, W_fc, b_fc, out):
             keep.tile([P, PASSES, CHANNELS], U8, name="edge_scales%d" % b, align_bytes=64) for b in batches
         ]
         waiting = {}
+        regrouped = []
 
+        bias_lone = const.tile([P, CHANNELS], BF16)
+        nc.vector.memset(bias_lone[:], 0.0)
+        nc.scalar.dma_start(out=bias_lone[0:1, :], in_=b_fc.unsqueeze(0))
+        ones = const.tile([P, P], BF16)
+        nc.vector.memset(ones[:], 1.0)
+        bias_row = const.tile([P, CHANNELS], BF16)
         w_sb = const.tile([P, CHUNKS, CHANNELS], BF16)
         w_t = const.tile([P, CHUNKS, CHANNELS], BF16)
         nc.sync.dma_start(out=x_sb[0][:, :, half(0)], in_=x_dram[0, :, :, half(0)])
@@ -89,8 +96,6 @@ def tile_hypercomputemodule_pa_kernel(tc, x, W_fc, b_fc, out):
         nc.sync.dma_start(out=x_sb[0][:, :, half(1)], in_=x_dram[0, :, :, half(1)])
         for hf in range(HALVES):
             nc.sync.dma_start(out=x_sb[1][:, :, half(hf)], in_=x_dram[1, :, :, half(hf)])
-        bias_row = const.tile([P, CHANNELS], BF16)
-        nc.scalar.dma_start(out=bias_row[:], in_=b_fc.partition_broadcast(P))
 
         ident_bf = const.tile([P, P], BF16)
         make_identity(nc, ident_bf[:])
@@ -121,6 +126,11 @@ def tile_hypercomputemodule_pa_kernel(tc, x, W_fc, b_fc, out):
                     nc.tensor.transpose(bank[:, block(ob)], w_sb[:, ob, block(cc)], ident_bf[:])
                 nc.vector.tensor_copy(out=w_t[:, cc, :], in_=bank[:])
 
+        def spread_bias():
+            bank = psum.tile([P, CHANNELS], F32, tag="bank")
+            nc.tensor.matmul(out=bank[:], lhsT=ones[:], rhs=bias_lone[:], start=True, stop=True)
+            nc.scalar.copy(out=bias_row[:], in_=bank[:])
+
         def half_norms(b):
             masked = stage.tile([P, BLOCKS, P], F32)
             nc.gpsimd.tensor_tensor(
@@ -140,13 +150,12 @@ def tile_hypercomputemodule_pa_kernel(tc, x, W_fc, b_fc, out):
                 op1=ALU.add,
             )
 
-        def spread(col, row):
-            for g in range(HALVES):
-                bank = psum.tile([P, PACK, P], F32, tag="bank")
-                for t in range(PACK):
-                    r = PACK * g + t
-                    nc.tensor.transpose(bank[:, t, :], col[:, r : r + 1].to_broadcast([P, P]), ident_f32[:])
-                nc.scalar.copy(out=row[:, half(g)], in_=bank[:].rearrange("p t n -> p (t n)"))
+        def spread(col, row, g):
+            bank = psum.tile([P, PACK, P], F32, tag="bank")
+            for t in range(PACK):
+                r = PACK * g + t
+                nc.tensor.transpose(bank[:, t, :], col[:, r : r + 1].to_broadcast([P, P]), ident_f32[:])
+            nc.scalar.copy(out=row[:, half(g)], in_=bank[:].rearrange("p t n -> p (t n)"))
 
         def compare(b, r, gram, cols, piece):
             nc.vector.scalar_tensor_tensor(
@@ -174,24 +183,22 @@ def tile_hypercomputemodule_pa_kernel(tc, x, W_fc, b_fc, out):
                 )
             compare(b, r, bank[:, :width], cols, 1 + hf)
 
-        def lower(b, r, hf):
-            first = hf * PACK
-            last = min(r, first + PACK)
-            bank = psum.tile([P, BANK], BF16, tag="bank")
-            for q in range(first, last):
-                nc.tensor.transpose(bank[:, block(q - first)], inc[b][:, q, block(r)], ident_bf[:])
+        def lower(b, r):
+            bank = psum.tile([P, PIXELS], BF16, tag="bank")
+            for q in range(r):
+                nc.tensor.transpose(bank[:, block(q)], inc[b][:, q, block(r)], ident_bf[:])
             nc.scalar.activation(
-                out=inc[b][:, r, first * P : last * P],
-                in_=bank[:, : (last - first) * P],
+                out=inc[b][:, r, : r * P],
+                in_=bank[:, : r * P],
                 func=ACT.Copy,
-                accum_out=deg_lower[b][:, r, 1 + hf : 2 + hf],
+                accum_out=deg_lower[b][:, r : r + 1],
             )
 
         def reciprocal_degrees(b):
-            both = stage.tile([P, BLOCKS, 1 + HALVES], F32)
-            nc.vector.tensor_tensor(out=both[:], in0=deg_upper[b][:], in1=deg_lower[b][:], op=ALU.add)
+            upper_sum = stage.tile([P, BLOCKS], F32)
+            nc.vector.tensor_reduce(out=upper_sum[:], in_=deg_upper[b][:], axis=AXIS.X, op=ALU.add)
             degree = stage.tile([P, BLOCKS], F32)
-            nc.vector.tensor_reduce(out=degree[:], in_=both[:], axis=AXIS.X, op=ALU.add)
+            nc.vector.tensor_tensor(out=degree[:], in0=upper_sum[:], in1=deg_lower[b][:], op=ALU.add)
             at_least_one = stage.tile([P, BLOCKS], F32)
             nc.vector.tensor_scalar_max(out=at_least_one[:], in0=degree[:], scalar1=1.0)
             nc.vector.reciprocal(out=r_col[b][:], in_=at_least_one[:])
@@ -208,38 +215,41 @@ def tile_hypercomputemodule_pa_kernel(tc, x, W_fc, b_fc, out):
         def regroup_incidence(engine_copy, b, g, hf):
             inc_grouped = stage.tile([P, BANK, PACK], BF16, align_bytes=64, bufs=INC_WAITING)
             regroup(engine_copy, inc_grouped[:], inc[b][:, PACK * g : PACK * (g + 1), half(hf)])
-            waiting[(b, g, hf)] = inc_grouped
+            regrouped.append((b, g, hf, inc_grouped))
 
-        def quantise_incidence(b, g, hf):
+        def quantise_oldest():
+            b, g, hf, inc_grouped = regrouped.pop(0)
             nc.vector.quantize_mx(
                 out=inc_codes[b][:, g, half(hf)].bitcast(FP8X4),
                 scales=inc_scales[b][:, g, half(hf)],
-                in_=waiting[(b, g, hf)][:].rearrange("p c t -> p (c t)"),
+                in_=inc_grouped[:].rearrange("p c t -> p (c t)"),
             )
 
-        def project(b, g):
-            xe_grouped = stage.tile([P, CHANNELS, PACK], BF16, align_bytes=64)
-            for ob in range(CHUNKS):
-                bank = psum.tile([P, PACK, P], F32, tag="bank")
-                for t in range(PACK):
-                    for cc in range(CHUNKS):
-                        nc.tensor.matmul(
-                            out=bank[:, t, :],
-                            lhsT=x_sb[b][:, cc, block(PACK * g + t)],
-                            rhs=w_t[:, cc, block(ob)],
-                            start=(cc == 0),
-                            stop=(cc == CHUNKS - 1),
-                        )
-                nc.vector.tensor_tensor(
-                    out=xe_grouped[:, block(ob), :],
-                    in0=bank[:].rearrange("p t o -> p o t"),
-                    in1=bias_row[:, block(ob)].unsqueeze(2).to_broadcast([P, P, PACK]),
-                    op=ALU.add,
-                )
+        def project(b, g, ob):
+            if ob == 0:
+                waiting[(b, g)] = stage.tile([P, CHANNELS, PACK], BF16, name="xe_grouped", align_bytes=64)
+            bank = psum.tile([P, PACK, P], F32, tag="bank")
+            for t in range(PACK):
+                for cc in range(CHUNKS):
+                    nc.tensor.matmul(
+                        out=bank[:, t, :],
+                        lhsT=x_sb[b][:, cc, block(PACK * g + t)],
+                        rhs=w_t[:, cc, block(ob)],
+                        start=(cc == 0),
+                        stop=(cc == CHUNKS - 1),
+                    )
+            nc.vector.tensor_tensor(
+                out=waiting[(b, g)][:, block(ob), :],
+                in0=bank[:].rearrange("p t o -> p o t"),
+                in1=bias_row[:, block(ob)].unsqueeze(2).to_broadcast([P, P, PACK]),
+                op=ALU.add,
+            )
+
+        def quantise_xe(b, g):
             nc.vector.quantize_mx(
                 out=xe_codes[b][:, g, :].bitcast(FP8X4),
                 scales=xe_scales[b][:, g, :],
-                in_=xe_grouped[:].rearrange("p o t -> p (o t)"),
+                in_=waiting[(b, g)][:].rearrange("p o t -> p (o t)"),
             )
 
         def edges(b, g_out):
@@ -284,10 +294,10 @@ def tile_hypercomputemodule_pa_kernel(tc, x, W_fc, b_fc, out):
                         stop=(g == PASSES - 1),
                     )
                 nc.scalar.activation(out=vert[:, t, :], in_=bank[:], func=ACT.Copy, scale=r_col[b][:, r : r + 1])
-            waiting[(b, hf)] = vert
+            waiting[(b, hf, "vert")] = vert
 
         def finish(b, hf):
-            vert = waiting[(b, hf)]
+            vert = waiting[(b, hf, "vert")]
             for ob in range(CHUNKS):
                 bank = psum.tile([P, PACK, P], F32, tag="bank")
                 for t in range(PACK):
@@ -305,69 +315,69 @@ def tile_hypercomputemodule_pa_kernel(tc, x, W_fc, b_fc, out):
             for r in range(BLOCKS):
                 compare(b, r, diag_sb[b][:, r, :], block(r), 0)
 
-        def square(b):
-            for r in range(PACK):
-                upper(b, r, 1)
-
-        def triangles(b):
-            for r in range(BLOCKS):
-                if r % PACK < PACK - 1:
-                    upper(b, r, r // PACK)
-
-        def mirror_square(b):
-            for r in range(PACK, BLOCKS):
-                lower(b, r, 0)
-
-        def mirror_triangles(b):
-            for r in range(BLOCKS):
-                if r % PACK > 0:
-                    lower(b, r, r // PACK)
+        def triangle(b, r):
+            if r % PACK < PACK - 1:
+                upper(b, r, r // PACK)
 
 
         gram_diagonal(0, 0)
         transpose_weights()
-        project(0, 0)
+        spread_bias()
+        for ob in range(CHUNKS):
+            project(0, 0, ob)
+        quantise_xe(0, 0)
         gram_diagonal(0, 1)
         gram_diagonal(1, 0)
         gram_diagonal(1, 1)
         half_norms(0)
-        project(0, 1)
+        for ob in range(CHUNKS):
+            project(0, 1, ob)
+        quantise_xe(0, 1)
         half_norms(1)
-        spread(h_col[0], h_row[0])
+        for g in range(HALVES):
+            spread(h_col[0], h_row[0], g)
 
         compare_diagonal(0)
-        square(0)
+        for r in range(PACK):
+            upper(0, r, 1)
+            if r >= HALVES:
+                spread(h_col[1], h_row[1], r - HALVES)
         regroup_incidence(gpsimd_copy, 0, 0, 1)
-        triangles(0)
-        spread(h_col[1], h_row[1])
-        mirror_square(0)
-        mirror_triangles(0)
-        quantise_incidence(0, 0, 1)
-        regroup_incidence(nc.scalar.copy, 0, 1, 0)
-        regroup_incidence(nc.scalar.copy, 0, 0, 0)
-        regroup_incidence(gpsimd_copy, 0, 1, 1)
+        for r in range(BLOCKS):
+            triangle(0, r)
 
         compare_diagonal(1)
-        square(1)
+        for r in range(PACK):
+            upper(1, r, 1)
+            lower(0, PACK + r)
+        quantise_oldest()
+        regroup_incidence(nc.scalar.copy, 0, 1, 0)
+        regroup_incidence(gpsimd_copy, 0, 1, 1)
+        for r in range(BLOCKS):
+            triangle(1, r)
+            if 0 < r < PACK:
+                lower(0, r)
+        regroup_incidence(nc.scalar.copy, 0, 0, 0)
         regroup_incidence(gpsimd_copy, 1, 0, 1)
-        quantise_incidence(0, 1, 0)
-        quantise_incidence(0, 1, 1)
-        triangles(1)
-        quantise_incidence(0, 0, 0)
         reciprocal_degrees(0)
-        mirror_square(1)
-        mirror_triangles(1)
-        quantise_incidence(1, 0, 1)
-        regroup_incidence(nc.scalar.copy, 1, 1, 0)
-        regroup_incidence(nc.scalar.copy, 1, 0, 0)
-        regroup_incidence(gpsimd_copy, 1, 1, 1)
 
-        project(1, 0)
-        quantise_incidence(1, 1, 0)
-        quantise_incidence(1, 1, 1)
+        for ob in range(CHUNKS):
+            project(1, 0, ob)
+            lower(1, PACK + ob)
+            quantise_oldest()
+        quantise_xe(1, 0)
+        regroup_incidence(nc.scalar.copy, 1, 1, 0)
+        for ob in range(CHUNKS):
+            project(1, 1, ob)
+            if ob > 0:
+                lower(1, ob)
+        quantise_xe(1, 1)
+        regroup_incidence(nc.vector.tensor_copy, 1, 0, 0)
+        regroup_incidence(gpsimd_copy, 1, 1, 1)
+        quantise_oldest()
         reciprocal_degrees(1)
-        project(1, 1)
-        quantise_incidence(1, 0, 0)
+        quantise_oldest()
+        quantise_oldest()
 
         for b in batches:
             for g_out in range(PASSES):

@@ -27,7 +27,15 @@ BLOCKS = PIXELS // P
 PASSES = PIXELS // K_PASS
 HALVES = PIXELS // BANK
 
-INC_WAITING = 6
+PIECE_DIAGONAL = 0
+PIECE_UPPER = 1
+PIECE_LOWER = PIECE_UPPER + HALVES
+PIECE_QUARTER = PIECE_LOWER + 1
+PIECES = PIECE_QUARTER + 1
+
+INC_WAITING = 5
+
+WARM_UP = 5
 
 FLOPS = BATCH * (2 * PIXELS * PIXELS * CHANNELS * 3 + 2 * PIXELS * CHANNELS * CHANNELS)
 
@@ -56,12 +64,12 @@ def tile_hypercomputemodule_pa_kernel(tc, x, W_fc, b_fc, out):
         batches = range(BATCH)
         x_sb = [keep.tile([P, CHUNKS, PIXELS], BF16, name="x_sb%d" % b) for b in batches]
         diag_sb = [keep.tile([P, BLOCKS, P], F32, name="diag_sb%d" % b) for b in batches]
+        sq_col = [keep.tile([P, BLOCKS], F32, name="sq_col%d" % b) for b in batches]
         h_col = [keep.tile([P, BLOCKS], F32, name="h_col%d" % b) for b in batches]
         h_row = [keep.tile([P, PIXELS], F32, name="h_row%d" % b) for b in batches]
         r_col = [keep.tile([P, BLOCKS], F32, name="r_col%d" % b) for b in batches]
         inc = [keep.tile([P, BLOCKS, PIXELS], BF16, name="inc%d" % b) for b in batches]
-        deg_upper = [keep.tile([P, BLOCKS, 1 + HALVES], F32, name="deg_upper%d" % b) for b in batches]
-        deg_lower = [keep.tile([P, BLOCKS], F32, name="deg_lower%d" % b) for b in batches]
+        degrees = [keep.tile([P, BLOCKS, PIECES], F32, name="degrees%d" % b) for b in batches]
         inc_codes = [
             keep.tile([P, PASSES, PIXELS], U32, name="inc_codes%d" % b, align_bytes=64) for b in batches
         ]
@@ -81,17 +89,18 @@ def tile_hypercomputemodule_pa_kernel(tc, x, W_fc, b_fc, out):
             keep.tile([P, PASSES, CHANNELS], U8, name="edge_scales%d" % b, align_bytes=64) for b in batches
         ]
         waiting = {}
-        regrouped = []
 
+        warm = const.tile([P, BANK], BF16)
+        nc.gpsimd.memset(warm[:], 0.0)
         bias_lone = const.tile([P, CHANNELS], BF16)
         nc.vector.memset(bias_lone[:], 0.0)
-        nc.scalar.dma_start(out=bias_lone[0:1, :], in_=b_fc.unsqueeze(0))
         ones = const.tile([P, P], BF16)
         nc.vector.memset(ones[:], 1.0)
         bias_row = const.tile([P, CHANNELS], BF16)
         w_sb = const.tile([P, CHUNKS, CHANNELS], BF16)
         w_t = const.tile([P, CHUNKS, CHANNELS], BF16)
         nc.sync.dma_start(out=x_sb[0][:, :, half(0)], in_=x_dram[0, :, :, half(0)])
+        nc.sync.dma_start(out=bias_lone[0:1, :], in_=b_fc.unsqueeze(0))
         nc.sync.dma_start(out=w_sb[:], in_=W_fc.rearrange("(ob p) c -> p ob c", p=P))
         nc.sync.dma_start(out=x_sb[0][:, :, half(1)], in_=x_dram[0, :, :, half(1)])
         for hf in range(HALVES):
@@ -102,8 +111,12 @@ def tile_hypercomputemodule_pa_kernel(tc, x, W_fc, b_fc, out):
         ident_f32 = const.tile([P, P], F32)
         make_identity(nc, ident_f32[:])
         for b in batches:
-            nc.vector.memset(deg_upper[b][:], 0.0)
-            nc.vector.memset(deg_lower[b][:], 0.0)
+            nc.vector.memset(degrees[b][:], 0.0)
+
+        def warm_up():
+            for i in range(WARM_UP):
+                bank = psum.tile([P, BANK], F32, tag="bank")
+                nc.tensor.matmul(out=bank[:], lhsT=warm[:, block(0)], rhs=warm[:], start=True, stop=True)
 
         def gram_diagonal(b, g):
             bank = psum.tile([P, PACK, P], F32, tag="bank")
@@ -131,19 +144,23 @@ def tile_hypercomputemodule_pa_kernel(tc, x, W_fc, b_fc, out):
             nc.tensor.matmul(out=bank[:], lhsT=ones[:], rhs=bias_lone[:], start=True, stop=True)
             nc.scalar.copy(out=bias_row[:], in_=bank[:])
 
-        def half_norms(b):
-            masked = stage.tile([P, BLOCKS, P], F32)
-            nc.gpsimd.tensor_tensor(
-                out=masked[:],
-                in0=diag_sb[b][:],
-                in1=ident_f32[:].unsqueeze(1).to_broadcast([P, BLOCKS, P]),
-                op=ALU.mult,
-            )
-            sq = stage.tile([P, BLOCKS], F32)
-            nc.vector.tensor_reduce(out=sq[:], in_=masked[:], axis=AXIS.X, op=ALU.add)
+        def half_norms(b, g):
+            blocks = slice(PACK * g, PACK * (g + 1))
+            masked = stage.tile([P, PACK, P], F32)
+            for t in range(PACK):
+                r = PACK * g + t
+                nc.vector.scalar_tensor_tensor(
+                    out=masked[:, t, :],
+                    in0=diag_sb[b][:, r, :],
+                    scalar=1.0,
+                    in1=ident_f32[:],
+                    op0=ALU.mult,
+                    op1=ALU.mult,
+                    accum_out=sq_col[b][:, r : r + 1],
+                )
             nc.vector.tensor_scalar(
-                out=h_col[b][:],
-                in0=sq[:],
+                out=h_col[b][:, blocks],
+                in0=sq_col[b][:, blocks],
                 scalar1=0.5,
                 scalar2=-THRESHOLD * THRESHOLD / 4.0,
                 op0=ALU.mult,
@@ -165,7 +182,7 @@ def tile_hypercomputemodule_pa_kernel(tc, x, W_fc, b_fc, out):
                 in1=h_row[b][:, cols],
                 op0=ALU.subtract,
                 op1=ALU.is_gt,
-                accum_out=deg_upper[b][:, r, piece : piece + 1],
+                accum_out=degrees[b][:, r, piece : piece + 1],
             )
 
         def upper(b, r, hf):
@@ -181,27 +198,74 @@ def tile_hypercomputemodule_pa_kernel(tc, x, W_fc, b_fc, out):
                     start=(cc == 0),
                     stop=(cc == CHUNKS - 1),
                 )
-            compare(b, r, bank[:, :width], cols, 1 + hf)
+            compare(b, r, bank[:, :width], cols, PIECE_UPPER + hf)
 
-        def lower(b, r):
-            bank = psum.tile([P, PIXELS], BF16, tag="bank")
-            for q in range(r):
-                nc.tensor.transpose(bank[:, block(q)], inc[b][:, q, block(r)], ident_bf[:])
-            nc.scalar.activation(
-                out=inc[b][:, r, : r * P],
-                in_=bank[:, : r * P],
-                func=ACT.Copy,
-                accum_out=deg_lower[b][:, r : r + 1],
+        def compare_diagonal(b, r):
+            compare(b, r, diag_sb[b][:, r, :], block(r), PIECE_DIAGONAL)
+
+        def triangle(b, r):
+            if r % PACK < PACK - 1:
+                upper(b, r, r // PACK)
+
+        def mirror_triangle(b, g):
+            for r in range(PACK * g + 1, PACK * (g + 1)):
+                first = PACK * g
+                width = (r - first) * P
+                bank = psum.tile([P, BANK], BF16, tag="bank")
+                for q in range(first, r):
+                    nc.tensor.transpose(bank[:, block(q - first)], inc[b][:, q, block(r)], ident_bf[:])
+                nc.scalar.activation(
+                    out=inc[b][:, r, first * P : first * P + width],
+                    in_=bank[:, :width],
+                    func=ACT.Copy,
+                    accum_out=degrees[b][:, r, PIECE_LOWER : PIECE_LOWER + 1],
+                )
+
+        def mirror_quarter(b, pair):
+            if pair == 0:
+                waiting[(b, 1, 0)] = stage.tile(
+                    [P, BANK, PACK], BF16, name="inc_grouped", align_bytes=64, bufs=INC_WAITING
+                )
+            grouped = waiting[(b, 1, 0)]
+            bank = psum.tile([P, 2, PACK, P], BF16, tag="bank")
+            for i in range(2):
+                q = 2 * pair + i
+                for t in range(PACK):
+                    nc.tensor.transpose(bank[:, i, t, :], inc[b][:, q, block(PACK + t)], ident_bf[:])
+            nc.scalar.copy(
+                out=grouped[:, 2 * P * pair : 2 * P * (pair + 1), :].rearrange("p (q c) t -> p q c t", q=2),
+                in_=bank[:].rearrange("p q t c -> p q c t"),
             )
 
-        def reciprocal_degrees(b):
-            upper_sum = stage.tile([P, BLOCKS], F32)
-            nc.vector.tensor_reduce(out=upper_sum[:], in_=deg_upper[b][:], axis=AXIS.X, op=ALU.add)
-            degree = stage.tile([P, BLOCKS], F32)
-            nc.vector.tensor_tensor(out=degree[:], in0=upper_sum[:], in1=deg_lower[b][:], op=ALU.add)
-            at_least_one = stage.tile([P, BLOCKS], F32)
-            nc.vector.tensor_scalar_max(out=at_least_one[:], in0=degree[:], scalar1=1.0)
-            nc.vector.reciprocal(out=r_col[b][:], in_=at_least_one[:])
+        def lower_degrees(b):
+            bank = psum.tile([P, PACK, 2], F32, tag="bank")
+            for t in range(PACK):
+                for q in range(PACK):
+                    nc.tensor.matmul(
+                        out=bank[:, t, :],
+                        lhsT=inc[b][:, q, block(PACK + t)],
+                        rhs=ones[:, 0:2],
+                        start=(q == 0),
+                        stop=(q == PACK - 1),
+                    )
+            nc.scalar.copy(
+                out=degrees[b][:, PACK : 2 * PACK, PIECE_QUARTER : PIECE_QUARTER + 1], in_=bank[:, :, 0:1]
+            )
+
+        def sum_degrees(b):
+            waiting[(b, "degree")] = stage.tile([P, BLOCKS], F32, name="degree")
+            nc.vector.tensor_reduce(
+                out=waiting[(b, "degree")][:], in_=degrees[b][:], axis=AXIS.X, op=ALU.add
+            )
+
+        def clamp_degrees(b):
+            waiting[(b, "clamped")] = stage.tile([P, BLOCKS], F32, name="clamped")
+            nc.vector.tensor_scalar_max(
+                out=waiting[(b, "clamped")][:], in0=waiting[(b, "degree")][:], scalar1=1.0
+            )
+
+        def invert_degrees(b):
+            nc.vector.reciprocal(out=r_col[b][:], in_=waiting[(b, "clamped")][:])
 
         def regroup(engine_copy, grouped, rows):
             engine_copy(
@@ -209,20 +273,16 @@ def tile_hypercomputemodule_pa_kernel(tc, x, W_fc, b_fc, out):
                 in_=rows.rearrange("p t (c i) -> p c t i", i=4),
             )
 
-        def gpsimd_copy(out, in_):
-            nc.gpsimd.tensor_scalar(out=out, in0=in_, scalar1=1.0, scalar2=0.0, op0=ALU.mult, op1=ALU.add)
-
         def regroup_incidence(engine_copy, b, g, hf):
-            inc_grouped = stage.tile([P, BANK, PACK], BF16, align_bytes=64, bufs=INC_WAITING)
-            regroup(engine_copy, inc_grouped[:], inc[b][:, PACK * g : PACK * (g + 1), half(hf)])
-            regrouped.append((b, g, hf, inc_grouped))
+            grouped = stage.tile([P, BANK, PACK], BF16, name="inc_grouped", align_bytes=64, bufs=INC_WAITING)
+            regroup(engine_copy, grouped[:], inc[b][:, PACK * g : PACK * (g + 1), half(hf)])
+            waiting[(b, g, hf)] = grouped
 
-        def quantise_oldest():
-            b, g, hf, inc_grouped = regrouped.pop(0)
+        def quantise_incidence(b, g, hf):
             nc.vector.quantize_mx(
                 out=inc_codes[b][:, g, half(hf)].bitcast(FP8X4),
                 scales=inc_scales[b][:, g, half(hf)],
-                in_=inc_grouped[:].rearrange("p c t -> p (c t)"),
+                in_=waiting[(b, g, hf)][:].rearrange("p c t -> p (c t)"),
             )
 
         def project(b, g, ob):
@@ -270,22 +330,48 @@ def tile_hypercomputemodule_pa_kernel(tc, x, W_fc, b_fc, out):
                 nc.scalar.activation(
                     out=edge_rows[:, t, :], in_=bank[:], func=ACT.Copy, scale=r_col[b][:, r : r + 1]
                 )
+            waiting[(b, g_out, "edge")] = edge_rows
+
+        def quantise_edges(b, g_out):
             edge_grouped = stage.tile([P, CHANNELS, PACK], BF16, align_bytes=64)
-            regroup(nc.vector.tensor_copy, edge_grouped[:], edge_rows[:])
+            regroup(nc.vector.tensor_copy, edge_grouped[:], waiting[(b, g_out, "edge")][:])
             nc.vector.quantize_mx(
                 out=edge_codes[b][:, g_out, :].bitcast(FP8X4),
                 scales=edge_scales[b][:, g_out, :],
                 in_=edge_grouped[:].rearrange("p o t -> p (o t)"),
             )
 
-        def vertices(b, hf):
-            vert = stage.tile([P, PACK, CHANNELS], F32)
-            for t in range(PACK):
-                r = PACK * hf + t
-                bank = psum.tile([P, CHANNELS], F32, tag="bank")
-                for g in range(PASSES):
+        def vertices(b, hf, t):
+            if t == 0:
+                waiting[(b, hf, "vert")] = stage.tile([P, PACK, CHANNELS], F32, name="vert", bufs=3)
+            r = PACK * hf + t
+            bank = psum.tile([P, CHANNELS], F32, tag="bank")
+            for g in range(PASSES):
+                nc.tensor.matmul_mx(
+                    out=bank[:],
+                    lhsT=inc_codes[b][:, g, block(r)].bitcast(FP8X4),
+                    lhsT_scale=inc_scales[b][:, g, block(r)],
+                    rhs=edge_codes[b][:, g, :].bitcast(FP8X4),
+                    rhs_scale=edge_scales[b][:, g, :],
+                    start=(g == 0),
+                    stop=(g == PASSES - 1),
+                )
+            nc.scalar.activation(
+                out=waiting[(b, hf, "vert")][:, t, :], in_=bank[:], func=ACT.Copy, scale=r_col[b][:, r : r + 1]
+            )
+
+        def vertices_by_pass(b, hf):
+            vert = stage.tile([P, PACK, CHANNELS], F32, name="vert", bufs=3)
+            waiting[(b, hf, "vert")] = vert
+            banks = []
+            for g in range(PASSES):
+                for t in range(PACK):
+                    r = PACK * hf + t
+                    if g == 0:
+                        bank = psum.tile([P, CHANNELS], F32, tag="bank")
+                        banks.append(bank)
                     nc.tensor.matmul_mx(
-                        out=bank[:],
+                        out=banks[t][:],
                         lhsT=inc_codes[b][:, g, block(r)].bitcast(FP8X4),
                         lhsT_scale=inc_scales[b][:, g, block(r)],
                         rhs=edge_codes[b][:, g, :].bitcast(FP8X4),
@@ -293,8 +379,11 @@ def tile_hypercomputemodule_pa_kernel(tc, x, W_fc, b_fc, out):
                         start=(g == 0),
                         stop=(g == PASSES - 1),
                     )
-                nc.scalar.activation(out=vert[:, t, :], in_=bank[:], func=ACT.Copy, scale=r_col[b][:, r : r + 1])
-            waiting[(b, hf, "vert")] = vert
+            for t in range(PACK):
+                r = PACK * hf + t
+                nc.scalar.activation(
+                    out=vert[:, t, :], in_=banks[t][:], func=ACT.Copy, scale=r_col[b][:, r : r + 1]
+                )
 
         def finish(b, hf):
             vert = waiting[(b, hf, "vert")]
@@ -311,82 +400,104 @@ def tile_hypercomputemodule_pa_kernel(tc, x, W_fc, b_fc, out):
                 )
                 nc.sync.dma_start(out=out_dram[b, :, ob, half(hf)], in_=result[:])
 
-        def compare_diagonal(b):
-            for r in range(BLOCKS):
-                compare(b, r, diag_sb[b][:, r, :], block(r), 0)
-
-        def triangle(b, r):
-            if r % PACK < PACK - 1:
-                upper(b, r, r // PACK)
-
-
+        warm_up()
         gram_diagonal(0, 0)
         transpose_weights()
         spread_bias()
-        for ob in range(CHUNKS):
-            project(0, 0, ob)
-        quantise_xe(0, 0)
         gram_diagonal(0, 1)
-        gram_diagonal(1, 0)
-        gram_diagonal(1, 1)
-        half_norms(0)
-        for ob in range(CHUNKS):
-            project(0, 1, ob)
-        quantise_xe(0, 1)
-        half_norms(1)
+        half_norms(0, 0)
+        project(0, 0, 0)
+        half_norms(0, 1)
+        for ob in range(1, CHUNKS):
+            project(0, 0, ob)
         for g in range(HALVES):
             spread(h_col[0], h_row[0], g)
+        quantise_xe(0, 0)
 
-        compare_diagonal(0)
         for r in range(PACK):
             upper(0, r, 1)
-            if r >= HALVES:
-                spread(h_col[1], h_row[1], r - HALVES)
-        regroup_incidence(gpsimd_copy, 0, 0, 1)
+            compare_diagonal(0, 2 * r)
+            compare_diagonal(0, 2 * r + 1)
+        regroup_incidence(nc.scalar.copy, 0, 0, 1)
         for r in range(BLOCKS):
             triangle(0, r)
 
-        compare_diagonal(1)
+        project(0, 1, 0)
+        mirror_quarter(0, 0)
+        quantise_incidence(0, 0, 1)
+        project(0, 1, 1)
+        mirror_quarter(0, 1)
+        lower_degrees(0)
+        project(0, 1, 2)
+        mirror_triangle(0, 0)
+        quantise_incidence(0, 1, 0)
+        project(0, 1, 3)
+        mirror_triangle(0, 1)
+        regroup_incidence(nc.vector.tensor_copy, 0, 0, 0)
+        quantise_xe(0, 1)
+        regroup_incidence(nc.vector.tensor_copy, 0, 1, 1)
+        quantise_incidence(0, 0, 0)
+        sum_degrees(0)
+
+        gram_diagonal(1, 0)
+        quantise_incidence(0, 1, 1)
+        clamp_degrees(0)
+        gram_diagonal(1, 1)
+        half_norms(1, 0)
+        invert_degrees(0)
+        project(1, 0, 0)
+        half_norms(1, 1)
+        for ob in range(1, CHUNKS):
+            project(1, 0, ob)
+        for g in range(HALVES):
+            spread(h_col[1], h_row[1], g)
+        quantise_xe(1, 0)
+
+        edges(0, 0)
+        edges(0, 1)
+        quantise_edges(0, 0)
         for r in range(PACK):
             upper(1, r, 1)
-            lower(0, PACK + r)
-        quantise_oldest()
-        regroup_incidence(nc.scalar.copy, 0, 1, 0)
-        regroup_incidence(gpsimd_copy, 0, 1, 1)
+            if r == 0:
+                quantise_edges(0, 1)
+            compare_diagonal(1, 2 * r)
+            compare_diagonal(1, 2 * r + 1)
+        regroup_incidence(nc.scalar.copy, 1, 0, 1)
         for r in range(BLOCKS):
             triangle(1, r)
-            if 0 < r < PACK:
-                lower(0, r)
-        regroup_incidence(nc.scalar.copy, 0, 0, 0)
-        regroup_incidence(gpsimd_copy, 1, 0, 1)
-        reciprocal_degrees(0)
-
-        for ob in range(CHUNKS):
-            project(1, 0, ob)
-            lower(1, PACK + ob)
-            quantise_oldest()
-        quantise_xe(1, 0)
-        regroup_incidence(nc.scalar.copy, 1, 1, 0)
-        for ob in range(CHUNKS):
-            project(1, 1, ob)
-            if ob > 0:
-                lower(1, ob)
-        quantise_xe(1, 1)
+        project(1, 1, 0)
+        mirror_quarter(1, 0)
+        quantise_incidence(1, 0, 1)
+        project(1, 1, 1)
+        mirror_quarter(1, 1)
+        lower_degrees(1)
+        project(1, 1, 2)
+        mirror_triangle(1, 0)
+        quantise_incidence(1, 1, 0)
+        project(1, 1, 3)
+        mirror_triangle(1, 1)
         regroup_incidence(nc.vector.tensor_copy, 1, 0, 0)
-        regroup_incidence(gpsimd_copy, 1, 1, 1)
-        quantise_oldest()
-        reciprocal_degrees(1)
-        quantise_oldest()
-        quantise_oldest()
+        quantise_xe(1, 1)
+        regroup_incidence(nc.vector.tensor_copy, 1, 1, 1)
+        quantise_incidence(1, 0, 0)
+        sum_degrees(1)
+        quantise_incidence(1, 1, 1)
+        clamp_degrees(1)
 
-        for b in batches:
-            for g_out in range(PASSES):
-                edges(b, g_out)
-        vertices(0, 0)
-        vertices(0, 1)
+        for hf in range(HALVES):
+            for t in range(PACK):
+                vertices(0, hf, t)
+        invert_degrees(1)
+        edges(1, 0)
         finish(0, 0)
-        vertices(1, 0)
+        edges(1, 1)
+        quantise_edges(1, 0)
+        quantise_edges(1, 1)
         finish(0, 1)
-        vertices(1, 1)
+        vertices_by_pass(1, 0)
+        for t in range(2):
+            vertices(1, 1, t)
         finish(1, 0)
+        for t in range(2, PACK):
+            vertices(1, 1, t)
         finish(1, 1)

@@ -31,7 +31,7 @@ PIECE_DIAGONAL = 0
 PIECE_UPPER = 1
 PIECE_LOWER = PIECE_UPPER + HALVES
 PIECE_QUARTER = PIECE_LOWER + 1
-PIECES = PIECE_QUARTER + 1
+PIECES = PIECE_QUARTER + 2
 
 INC_WAITING = 5
 
@@ -67,6 +67,7 @@ def tile_hypercomputemodule_pa_kernel(tc, x, W_fc, b_fc, out):
         sq_col = [keep.tile([P, BLOCKS], F32, name="sq_col%d" % b) for b in batches]
         h_col = [keep.tile([P, BLOCKS], F32, name="h_col%d" % b) for b in batches]
         h_row = [keep.tile([P, PIXELS], F32, name="h_row%d" % b) for b in batches]
+        r_row = [keep.tile([P, PIXELS], F32, name="r_row%d" % b) for b in range(1)]
         r_col = [keep.tile([P, BLOCKS], F32, name="r_col%d" % b) for b in batches]
         inc = [keep.tile([P, BLOCKS, PIXELS], BF16, name="inc%d" % b) for b in batches]
         degrees = [keep.tile([P, BLOCKS, PIECES], F32, name="degrees%d" % b) for b in batches]
@@ -91,16 +92,16 @@ def tile_hypercomputemodule_pa_kernel(tc, x, W_fc, b_fc, out):
         waiting = {}
 
         warm = const.tile([P, BANK], BF16)
-        nc.gpsimd.memset(warm[:], 0.0)
         bias_lone = const.tile([P, CHANNELS], BF16)
-        nc.vector.memset(bias_lone[:], 0.0)
+        nc.gpsimd.memset(bias_lone[:], 0.0)
+        nc.vector.memset(warm[:], 0.0)
         ones = const.tile([P, P], BF16)
         nc.vector.memset(ones[:], 1.0)
+        nc.scalar.dma_start(out=bias_lone[0:1, :], in_=b_fc.unsqueeze(0))
         bias_row = const.tile([P, CHANNELS], BF16)
         w_sb = const.tile([P, CHUNKS, CHANNELS], BF16)
         w_t = const.tile([P, CHUNKS, CHANNELS], BF16)
         nc.sync.dma_start(out=x_sb[0][:, :, half(0)], in_=x_dram[0, :, :, half(0)])
-        nc.sync.dma_start(out=bias_lone[0:1, :], in_=b_fc.unsqueeze(0))
         nc.sync.dma_start(out=w_sb[:], in_=W_fc.rearrange("(ob p) c -> p ob c", p=P))
         nc.sync.dma_start(out=x_sb[0][:, :, half(1)], in_=x_dram[0, :, :, half(1)])
         for hf in range(HALVES):
@@ -236,21 +237,14 @@ def tile_hypercomputemodule_pa_kernel(tc, x, W_fc, b_fc, out):
                 out=grouped[:, 2 * P * pair : 2 * P * (pair + 1), :].rearrange("p (q c) t -> p q c t", q=2),
                 in_=bank[:].rearrange("p q t c -> p q c t"),
             )
-
-        def lower_degrees(b):
-            bank = psum.tile([P, PACK, 2], F32, tag="bank")
             for t in range(PACK):
-                for q in range(PACK):
-                    nc.tensor.matmul(
-                        out=bank[:, t, :],
-                        lhsT=inc[b][:, q, block(PACK + t)],
-                        rhs=ones[:, 0:2],
-                        start=(q == 0),
-                        stop=(q == PACK - 1),
-                    )
-            nc.scalar.copy(
-                out=degrees[b][:, PACK : 2 * PACK, PIECE_QUARTER : PIECE_QUARTER + 1], in_=bank[:, :, 0:1]
-            )
+                summed = stage.tile([P, 2, P], BF16)
+                nc.scalar.activation(
+                    out=summed[:],
+                    in_=bank[:, :, t, :],
+                    func=ACT.Copy,
+                    accum_out=degrees[b][:, PACK + t, PIECE_QUARTER + pair : PIECE_QUARTER + pair + 1],
+                )
 
         def sum_degrees(b):
             waiting[(b, "degree")] = stage.tile([P, BLOCKS], F32, name="degree")
@@ -312,7 +306,13 @@ def tile_hypercomputemodule_pa_kernel(tc, x, W_fc, b_fc, out):
                 in_=waiting[(b, g)][:].rearrange("p o t -> p (o t)"),
             )
 
-        def edges(b, g_out):
+        def scale_rows(on_vector, out, sums, b, r):
+            if on_vector:
+                nc.vector.tensor_scalar_mul(out=out, in0=sums, scalar1=r_col[b][:, r : r + 1])
+            else:
+                nc.scalar.activation(out=out, in_=sums, func=ACT.Copy, scale=r_col[b][:, r : r + 1])
+
+        def edges(b, g_out, on_vector=()):
             edge_rows = stage.tile([P, PACK, CHANNELS], BF16)
             for t in range(PACK):
                 r = PACK * g_out + t
@@ -327,21 +327,23 @@ def tile_hypercomputemodule_pa_kernel(tc, x, W_fc, b_fc, out):
                         start=(g == 0),
                         stop=(g == PASSES - 1),
                     )
-                nc.scalar.activation(
-                    out=edge_rows[:, t, :], in_=bank[:], func=ACT.Copy, scale=r_col[b][:, r : r + 1]
-                )
+                scale_rows(t in on_vector, edge_rows[:, t, :], bank[:], b, r)
             waiting[(b, g_out, "edge")] = edge_rows
 
-        def quantise_edges(b, g_out):
+        def regroup_edges(engine_copy, b, g_out):
             edge_grouped = stage.tile([P, CHANNELS, PACK], BF16, align_bytes=64)
-            regroup(nc.vector.tensor_copy, edge_grouped[:], waiting[(b, g_out, "edge")][:])
+            regroup(engine_copy, edge_grouped[:], waiting[(b, g_out, "edge")][:])
+            waiting[(b, g_out, "edge grouped")] = edge_grouped
+
+        def quantise_edges(b, g_out):
+            edge_grouped = waiting[(b, g_out, "edge grouped")]
             nc.vector.quantize_mx(
                 out=edge_codes[b][:, g_out, :].bitcast(FP8X4),
                 scales=edge_scales[b][:, g_out, :],
                 in_=edge_grouped[:].rearrange("p o t -> p (o t)"),
             )
 
-        def vertices(b, hf, t):
+        def vertices(b, hf, t, on_vector=False):
             if t == 0:
                 waiting[(b, hf, "vert")] = stage.tile([P, PACK, CHANNELS], F32, name="vert", bufs=3)
             r = PACK * hf + t
@@ -356,11 +358,32 @@ def tile_hypercomputemodule_pa_kernel(tc, x, W_fc, b_fc, out):
                     start=(g == 0),
                     stop=(g == PASSES - 1),
                 )
-            nc.scalar.activation(
-                out=waiting[(b, hf, "vert")][:, t, :], in_=bank[:], func=ACT.Copy, scale=r_col[b][:, r : r + 1]
-            )
+            scale_rows(on_vector, waiting[(b, hf, "vert")][:, t, :], bank[:], b, r)
 
-        def vertices_by_pass(b, hf):
+        def vertices_turned(b, hf, ob):
+            bank = psum.tile([P, BANK], F32, tag="bank")
+            for g in range(PASSES):
+                nc.tensor.matmul_mx(
+                    out=bank[:],
+                    lhsT=edge_codes[b][:, g, block(ob)].bitcast(FP8X4),
+                    lhsT_scale=edge_scales[b][:, g, block(ob)],
+                    rhs=inc_codes[b][:, g, half(hf)].bitcast(FP8X4),
+                    rhs_scale=inc_scales[b][:, g, half(hf)],
+                    start=(g == 0),
+                    stop=(g == PASSES - 1),
+                )
+            scaled = results.tile([P, BANK], F32, name="scaled", bufs=5)
+            nc.vector.tensor_tensor(out=scaled[:], in0=bank[:], in1=r_row[b][:, half(hf)], op=ALU.mult)
+            waiting[(b, hf, ob, "scaled")] = scaled
+
+        def add_residual(engine, b, hf, ob):
+            result = results.tile([P, BANK], F32, name="result")
+            engine.tensor_tensor(
+                out=result[:], in0=waiting[(b, hf, ob, "scaled")][:], in1=x_sb[b][:, ob, half(hf)], op=ALU.add
+            )
+            nc.sync.dma_start(out=out_dram[b, :, ob, half(hf)], in_=result[:])
+
+        def vertices_by_pass(b, hf, on_vector=()):
             vert = stage.tile([P, PACK, CHANNELS], F32, name="vert", bufs=3)
             waiting[(b, hf, "vert")] = vert
             banks = []
@@ -381,33 +404,37 @@ def tile_hypercomputemodule_pa_kernel(tc, x, W_fc, b_fc, out):
                     )
             for t in range(PACK):
                 r = PACK * hf + t
-                nc.scalar.activation(
-                    out=vert[:, t, :], in_=banks[t][:], func=ACT.Copy, scale=r_col[b][:, r : r + 1]
-                )
+                scale_rows(t in on_vector, vert[:, t, :], banks[t][:], b, r)
 
-        def finish(b, hf):
+        def finish(b, hf, first, count):
             vert = waiting[(b, hf, "vert")]
+            width = count * P
+            pixels = slice(hf * BANK + first * P, hf * BANK + first * P + width)
             for ob in range(CHUNKS):
                 bank = psum.tile([P, PACK, P], F32, tag="bank")
-                for t in range(PACK):
-                    nc.tensor.transpose(bank[:, t, :], vert[:, t, block(ob)], ident_f32[:])
-                result = results.tile([P, BANK], F32)
+                for t in range(count):
+                    nc.tensor.transpose(bank[:, t, :], vert[:, first + t, block(ob)], ident_f32[:])
+                result = results.tile([P, BANK], F32, name="result")
                 nc.vector.tensor_tensor(
-                    out=result[:],
-                    in0=bank[:].rearrange("p t i -> p (t i)"),
-                    in1=x_sb[b][:, ob, half(hf)],
+                    out=result[:, :width],
+                    in0=bank[:, :count, :].rearrange("p t i -> p (t i)"),
+                    in1=x_sb[b][:, ob, pixels],
                     op=ALU.add,
                 )
-                nc.sync.dma_start(out=out_dram[b, :, ob, half(hf)], in_=result[:])
+                nc.sync.dma_start(out=out_dram[b, :, ob, pixels], in_=result[:, :width])
 
         warm_up()
+        spread_bias()
         gram_diagonal(0, 0)
         transpose_weights()
-        spread_bias()
         gram_diagonal(0, 1)
         half_norms(0, 0)
-        project(0, 0, 0)
+        gram_diagonal(1, 0)
         half_norms(0, 1)
+        gram_diagonal(1, 1)
+        half_norms(1, 0)
+        project(0, 0, 0)
+        half_norms(1, 1)
         for ob in range(1, CHUNKS):
             project(0, 0, ob)
         for g in range(HALVES):
@@ -424,80 +451,89 @@ def tile_hypercomputemodule_pa_kernel(tc, x, W_fc, b_fc, out):
 
         project(0, 1, 0)
         mirror_quarter(0, 0)
-        quantise_incidence(0, 0, 1)
         project(0, 1, 1)
         mirror_quarter(0, 1)
-        lower_degrees(0)
+        quantise_incidence(0, 0, 1)
         project(0, 1, 2)
         mirror_triangle(0, 0)
-        quantise_incidence(0, 1, 0)
         project(0, 1, 3)
         mirror_triangle(0, 1)
-        regroup_incidence(nc.vector.tensor_copy, 0, 0, 0)
-        quantise_xe(0, 1)
-        regroup_incidence(nc.vector.tensor_copy, 0, 1, 1)
-        quantise_incidence(0, 0, 0)
-        sum_degrees(0)
-
-        gram_diagonal(1, 0)
-        quantise_incidence(0, 1, 1)
-        clamp_degrees(0)
-        gram_diagonal(1, 1)
-        half_norms(1, 0)
-        invert_degrees(0)
-        project(1, 0, 0)
-        half_norms(1, 1)
-        for ob in range(1, CHUNKS):
-            project(1, 0, ob)
         for g in range(HALVES):
             spread(h_col[1], h_row[1], g)
-        quantise_xe(1, 0)
+        quantise_incidence(0, 1, 0)
+        quantise_xe(0, 1)
+        regroup_incidence(nc.scalar.copy, 0, 0, 0)
+        regroup_incidence(nc.scalar.copy, 0, 1, 1)
 
-        edges(0, 0)
-        edges(0, 1)
-        quantise_edges(0, 0)
         for r in range(PACK):
             upper(1, r, 1)
-            if r == 0:
-                quantise_edges(0, 1)
+            if r == 1:
+                sum_degrees(0)
+            if r == 2:
+                quantise_incidence(0, 0, 0)
+                clamp_degrees(0)
             compare_diagonal(1, 2 * r)
             compare_diagonal(1, 2 * r + 1)
         regroup_incidence(nc.scalar.copy, 1, 0, 1)
         for r in range(BLOCKS):
             triangle(1, r)
-        project(1, 1, 0)
+            if r == 0:
+                invert_degrees(0)
+                quantise_incidence(0, 1, 1)
+        project(1, 0, 0)
         mirror_quarter(1, 0)
-        quantise_incidence(1, 0, 1)
-        project(1, 1, 1)
+        project(1, 0, 1)
         mirror_quarter(1, 1)
-        lower_degrees(1)
-        project(1, 1, 2)
+        quantise_incidence(1, 0, 1)
+        project(1, 0, 2)
         mirror_triangle(1, 0)
-        quantise_incidence(1, 1, 0)
-        project(1, 1, 3)
+        project(1, 0, 3)
         mirror_triangle(1, 1)
-        regroup_incidence(nc.vector.tensor_copy, 1, 0, 0)
-        quantise_xe(1, 1)
-        regroup_incidence(nc.vector.tensor_copy, 1, 1, 1)
-        quantise_incidence(1, 0, 0)
-        sum_degrees(1)
-        quantise_incidence(1, 1, 1)
-        clamp_degrees(1)
+        quantise_xe(1, 0)
+        quantise_incidence(1, 1, 0)
 
-        for hf in range(HALVES):
-            for t in range(PACK):
-                vertices(0, hf, t)
+        edges(0, 0)
+        regroup_incidence(nc.vector.tensor_copy, 1, 0, 0)
+        edges(0, 1)
+        regroup_edges(nc.scalar.copy, 0, 1)
+        regroup_edges(nc.vector.tensor_copy, 0, 0)
+        quantise_incidence(1, 0, 0)
+        quantise_edges(0, 0)
+        for ob in range(CHUNKS):
+            if ob == 3:
+                quantise_edges(0, 1)
+            project(1, 1, ob)
+            if ob == 1:
+                sum_degrees(1)
+            if ob == 2:
+                clamp_degrees(1)
+        for g in range(HALVES):
+            spread(r_col[0], r_row[0], g)
+        regroup_incidence(nc.scalar.copy, 1, 1, 1)
+        quantise_xe(1, 1)
         invert_degrees(1)
+        for ob in range(CHUNKS):
+            vertices_turned(0, 0, ob)
+            if ob == 2:
+                quantise_incidence(1, 1, 1)
         edges(1, 0)
-        finish(0, 0)
-        edges(1, 1)
+        for ob in range(CHUNKS):
+            add_residual(nc.gpsimd, 0, 0, ob)
+        regroup_edges(nc.vector.tensor_copy, 1, 0)
+        edges(1, 1, (3,))
         quantise_edges(1, 0)
+        regroup_edges(nc.vector.tensor_copy, 1, 1)
+        vertices_turned(0, 1, 0)
         quantise_edges(1, 1)
-        finish(0, 1)
-        vertices_by_pass(1, 0)
-        for t in range(2):
-            vertices(1, 1, t)
-        finish(1, 0)
-        for t in range(2, PACK):
-            vertices(1, 1, t)
-        finish(1, 1)
+        for ob in range(1, CHUNKS):
+            vertices_turned(0, 1, ob)
+        vertices_by_pass(1, 0, (1, 3))
+        for ob in range(CHUNKS):
+            add_residual(nc.gpsimd, 0, 1, ob)
+        vertices(1, 1, 0)
+        vertices(1, 1, 1)
+        finish(1, 0, 0, 4)
+        vertices(1, 1, 2)
+        vertices(1, 1, 3)
+        finish(1, 1, 0, 2)
+        finish(1, 1, 2, 2)

@@ -35,7 +35,7 @@ PIECES = PIECE_QUARTER + 2
 
 INC_WAITING = 5
 
-WARM_UP = 5
+WARM_UP = 3
 
 FLOPS = BATCH * (2 * PIXELS * PIXELS * CHANNELS * 3 + 2 * PIXELS * CHANNELS * CHANNELS)
 
@@ -97,11 +97,12 @@ def tile_hypercomputemodule_pa_kernel(tc, x, W_fc, b_fc, out):
         nc.vector.memset(warm[:], 0.0)
         ones = const.tile([P, P], BF16)
         nc.vector.memset(ones[:], 1.0)
-        nc.scalar.dma_start(out=bias_lone[0:1, :], in_=b_fc.unsqueeze(0))
         bias_row = const.tile([P, CHANNELS], BF16)
         w_sb = const.tile([P, CHUNKS, CHANNELS], BF16)
         w_t = const.tile([P, CHUNKS, CHANNELS], BF16)
-        nc.sync.dma_start(out=x_sb[0][:, :, half(0)], in_=x_dram[0, :, :, half(0)])
+        for cc in range(CHUNKS):
+            nc.sync.dma_start(out=x_sb[0][:, cc, half(0)], in_=x_dram[0, :, cc, half(0)])
+        nc.sync.dma_start(out=bias_lone[0:1, :], in_=b_fc.unsqueeze(0))
         nc.sync.dma_start(out=w_sb[:], in_=W_fc.rearrange("(ob p) c -> p ob c", p=P))
         nc.sync.dma_start(out=x_sb[0][:, :, half(1)], in_=x_dram[0, :, :, half(1)])
         for hf in range(HALVES):
@@ -132,6 +133,24 @@ def tile_hypercomputemodule_pa_kernel(tc, x, W_fc, b_fc, out):
                         stop=(cc == CHUNKS - 1),
                     )
             nc.scalar.copy(out=diag_sb[b][:, PACK * g : PACK * (g + 1), :], in_=bank[:])
+
+        def gram_diagonal_by_chunk(b, g):
+            banks = []
+            for cc in range(CHUNKS):
+                for t in range(PACK):
+                    rows = block(PACK * g + t)
+                    if cc == 0:
+                        bank = psum.tile([P, P], F32, tag="bank")
+                        banks.append(bank)
+                    nc.tensor.matmul(
+                        out=banks[t][:],
+                        lhsT=x_sb[b][:, cc, rows],
+                        rhs=x_sb[b][:, cc, rows],
+                        start=(cc == 0),
+                        stop=(cc == CHUNKS - 1),
+                    )
+            for t in range(PACK):
+                nc.scalar.copy(out=diag_sb[b][:, PACK * g + t, :], in_=banks[t][:])
 
         def transpose_weights():
             for cc in range(CHUNKS):
@@ -424,9 +443,9 @@ def tile_hypercomputemodule_pa_kernel(tc, x, W_fc, b_fc, out):
                 nc.sync.dma_start(out=out_dram[b, :, ob, pixels], in_=result[:, :width])
 
         warm_up()
-        spread_bias()
-        gram_diagonal(0, 0)
+        gram_diagonal_by_chunk(0, 0)
         transpose_weights()
+        spread_bias()
         gram_diagonal(0, 1)
         half_norms(0, 0)
         gram_diagonal(1, 0)

@@ -65,9 +65,8 @@ def tile_hypercomputemodule_pa_kernel(tc, x, W_fc, b_fc, out):
         x_sb = [keep.tile([P, CHUNKS, PIXELS], BF16, name="x_sb%d" % b) for b in batches]
         diag_sb = [keep.tile([P, BLOCKS, P], F32, name="diag_sb%d" % b) for b in batches]
         sq_col = [keep.tile([P, BLOCKS], F32, name="sq_col%d" % b) for b in batches]
-        h_col = [keep.tile([P, BLOCKS], F32, name="h_col%d" % b) for b in batches]
+        h_col = [keep.tile([P, P], F32, name="h_col%d" % b) for b in batches]
         h_row = [keep.tile([P, PIXELS], F32, name="h_row%d" % b) for b in batches]
-        r_row = [keep.tile([P, PIXELS], F32, name="r_row%d" % b) for b in range(1)]
         r_col = [keep.tile([P, BLOCKS], F32, name="r_col%d" % b) for b in batches]
         inc = [keep.tile([P, BLOCKS, PIXELS], BF16, name="inc%d" % b) for b in batches]
         degrees = [keep.tile([P, BLOCKS, PIECES], F32, name="degrees%d" % b) for b in batches]
@@ -92,21 +91,17 @@ def tile_hypercomputemodule_pa_kernel(tc, x, W_fc, b_fc, out):
         waiting = {}
 
         warm = const.tile([P, BANK], BF16)
-        bias_lone = const.tile([P, CHANNELS], BF16)
-        nc.gpsimd.memset(bias_lone[:], 0.0)
         nc.vector.memset(warm[:], 0.0)
-        ones = const.tile([P, P], BF16)
-        nc.vector.memset(ones[:], 1.0)
         bias_row = const.tile([P, CHANNELS], BF16)
         w_sb = const.tile([P, CHUNKS, CHANNELS], BF16)
         w_t = const.tile([P, CHUNKS, CHANNELS], BF16)
         for cc in range(CHUNKS):
             nc.sync.dma_start(out=x_sb[0][:, cc, half(0)], in_=x_dram[0, :, cc, half(0)])
-        nc.sync.dma_start(out=bias_lone[0:1, :], in_=b_fc.unsqueeze(0))
-        nc.sync.dma_start(out=w_sb[:], in_=W_fc.rearrange("(ob p) c -> p ob c", p=P))
         nc.sync.dma_start(out=x_sb[0][:, :, half(1)], in_=x_dram[0, :, :, half(1)])
         for hf in range(HALVES):
             nc.sync.dma_start(out=x_sb[1][:, :, half(hf)], in_=x_dram[1, :, :, half(hf)])
+        nc.sync.dma_start(out=w_sb[:], in_=W_fc.rearrange("(ob p) c -> p ob c", p=P))
+        nc.sync.dma_start(out=bias_row[:], in_=b_fc.partition_broadcast(P))
 
         ident_bf = const.tile([P, P], BF16)
         make_identity(nc, ident_bf[:])
@@ -114,6 +109,7 @@ def tile_hypercomputemodule_pa_kernel(tc, x, W_fc, b_fc, out):
         make_identity(nc, ident_f32[:])
         for b in batches:
             nc.vector.memset(degrees[b][:], 0.0)
+        nc.gpsimd.memset(h_col[1][:], 0.0)
 
         def warm_up():
             for i in range(WARM_UP):
@@ -157,12 +153,7 @@ def tile_hypercomputemodule_pa_kernel(tc, x, W_fc, b_fc, out):
                 bank = psum.tile([P, CHANNELS], BF16, tag="bank")
                 for ob in range(CHUNKS):
                     nc.tensor.transpose(bank[:, block(ob)], w_sb[:, ob, block(cc)], ident_bf[:])
-                nc.vector.tensor_copy(out=w_t[:, cc, :], in_=bank[:])
-
-        def spread_bias():
-            bank = psum.tile([P, CHANNELS], F32, tag="bank")
-            nc.tensor.matmul(out=bank[:], lhsT=ones[:], rhs=bias_lone[:], start=True, stop=True)
-            nc.scalar.copy(out=bias_row[:], in_=bank[:])
+                nc.scalar.copy(out=w_t[:, cc, :], in_=bank[:])
 
         def half_norms(b, g):
             blocks = slice(PACK * g, PACK * (g + 1))
@@ -193,6 +184,18 @@ def tile_hypercomputemodule_pa_kernel(tc, x, W_fc, b_fc, out):
                 r = PACK * g + t
                 nc.tensor.transpose(bank[:, t, :], col[:, r : r + 1].to_broadcast([P, P]), ident_f32[:])
             nc.scalar.copy(out=row[:, half(g)], in_=bank[:].rearrange("p t n -> p (t n)"))
+
+        def park(col, channel):
+            bank = psum.tile([P, P], F32, tag="bank")
+            nc.tensor.transpose(bank[:], col[:], ident_f32[:])
+            line = stage.tile([BLOCKS, P], F32)
+            nc.scalar.copy(out=line[:], in_=bank[:BLOCKS, :])
+            parked = out[BATCH - 1, channel].rearrange("h w -> (h w)")
+            nc.sync.dma_start(out=parked.rearrange("(r p) -> r p", p=P), in_=line[:])
+            return parked
+
+        def fetch(row, parked):
+            nc.sync.dma_start(out=row[:], in_=parked.partition_broadcast(P))
 
         def compare(b, r, gram, cols, piece):
             nc.vector.scalar_tensor_tensor(
@@ -256,15 +259,12 @@ def tile_hypercomputemodule_pa_kernel(tc, x, W_fc, b_fc, out):
                 out=grouped[:, 2 * P * pair : 2 * P * (pair + 1), :].rearrange("p (q c) t -> p q c t", q=2),
                 in_=bank[:].rearrange("p q t c -> p q c t"),
             )
-            for t in range(PACK):
-                summed = stage.tile([P, 2, P], BF16)
-                nc.scalar.activation(
-                    out=summed[:],
-                    in_=bank[:, :, t, :],
-                    func=ACT.Copy,
-                    accum_out=degrees[b][:, PACK + t, PIECE_QUARTER + pair : PIECE_QUARTER + pair + 1],
-                )
-
+            nc.vector.tensor_reduce(
+                out=degrees[b][:, PACK : 2 * PACK, PIECE_QUARTER + pair],
+                in_=bank[:].rearrange("p q t c -> p t q c"),
+                axis=AXIS.XY,
+                op=ALU.add,
+            )
         def sum_degrees(b):
             waiting[(b, "degree")] = stage.tile([P, BLOCKS], F32, name="degree")
             nc.vector.tensor_reduce(
@@ -349,8 +349,34 @@ def tile_hypercomputemodule_pa_kernel(tc, x, W_fc, b_fc, out):
                 scale_rows(t in on_vector, edge_rows[:, t, :], bank[:], b, r)
             waiting[(b, g_out, "edge")] = edge_rows
 
+        def edges_by_word(b, g_out, obs):
+            if 0 in obs:
+                waiting[(b, g_out, "edge grouped")] = stage.tile(
+                    [P, CHANNELS, PACK], BF16, name="edge_grouped", align_bytes=64
+                )
+            for ob in obs:
+                bank = psum.tile([P, PACK, P], F32, tag="bank")
+                for t in range(PACK):
+                    r = PACK * g_out + t
+                    for g in range(PASSES):
+                        nc.tensor.matmul_mx(
+                            out=bank[:, t, :],
+                            lhsT=inc_codes[b][:, g, block(r)].bitcast(FP8X4),
+                            lhsT_scale=inc_scales[b][:, g, block(r)],
+                            rhs=xe_codes[b][:, g, block(ob)].bitcast(FP8X4),
+                            rhs_scale=xe_scales[b][:, g, block(ob)],
+                            start=(g == 0),
+                            stop=(g == PASSES - 1),
+                        )
+                nc.vector.tensor_tensor(
+                    out=waiting[(b, g_out, "edge grouped")][:, block(ob), :],
+                    in0=bank[:].rearrange("p t o -> p o t"),
+                    in1=r_col[b][:, PACK * g_out : PACK * (g_out + 1)].unsqueeze(1).to_broadcast([P, P, PACK]),
+                    op=ALU.mult,
+                )
+
         def regroup_edges(engine_copy, b, g_out):
-            edge_grouped = stage.tile([P, CHANNELS, PACK], BF16, align_bytes=64)
+            edge_grouped = stage.tile([P, CHANNELS, PACK], BF16, name="edge_grouped", align_bytes=64)
             regroup(engine_copy, edge_grouped[:], waiting[(b, g_out, "edge")][:])
             waiting[(b, g_out, "edge grouped")] = edge_grouped
 
@@ -378,29 +404,6 @@ def tile_hypercomputemodule_pa_kernel(tc, x, W_fc, b_fc, out):
                     stop=(g == PASSES - 1),
                 )
             scale_rows(on_vector, waiting[(b, hf, "vert")][:, t, :], bank[:], b, r)
-
-        def vertices_turned(b, hf, ob):
-            bank = psum.tile([P, BANK], F32, tag="bank")
-            for g in range(PASSES):
-                nc.tensor.matmul_mx(
-                    out=bank[:],
-                    lhsT=edge_codes[b][:, g, block(ob)].bitcast(FP8X4),
-                    lhsT_scale=edge_scales[b][:, g, block(ob)],
-                    rhs=inc_codes[b][:, g, half(hf)].bitcast(FP8X4),
-                    rhs_scale=inc_scales[b][:, g, half(hf)],
-                    start=(g == 0),
-                    stop=(g == PASSES - 1),
-                )
-            scaled = results.tile([P, BANK], F32, name="scaled", bufs=5)
-            nc.vector.tensor_tensor(out=scaled[:], in0=bank[:], in1=r_row[b][:, half(hf)], op=ALU.mult)
-            waiting[(b, hf, ob, "scaled")] = scaled
-
-        def add_residual(engine, b, hf, ob):
-            result = results.tile([P, BANK], F32, name="result")
-            engine.tensor_tensor(
-                out=result[:], in0=waiting[(b, hf, ob, "scaled")][:], in1=x_sb[b][:, ob, half(hf)], op=ALU.add
-            )
-            nc.sync.dma_start(out=out_dram[b, :, ob, half(hf)], in_=result[:])
 
         def vertices_by_pass(b, hf, on_vector=()):
             vert = stage.tile([P, PACK, CHANNELS], F32, name="vert", bufs=3)
@@ -444,111 +447,104 @@ def tile_hypercomputemodule_pa_kernel(tc, x, W_fc, b_fc, out):
 
         warm_up()
         gram_diagonal_by_chunk(0, 0)
-        transpose_weights()
-        spread_bias()
         gram_diagonal(0, 1)
         half_norms(0, 0)
         gram_diagonal(1, 0)
         half_norms(0, 1)
         gram_diagonal(1, 1)
-        half_norms(1, 0)
-        project(0, 0, 0)
-        half_norms(1, 1)
-        for ob in range(1, CHUNKS):
-            project(0, 0, ob)
         for g in range(HALVES):
             spread(h_col[0], h_row[0], g)
-        quantise_xe(0, 0)
+        half_norms(1, 0)
 
         for r in range(PACK):
             upper(0, r, 1)
             compare_diagonal(0, 2 * r)
             compare_diagonal(0, 2 * r + 1)
+        transpose_weights()
         regroup_incidence(nc.scalar.copy, 0, 0, 1)
         for r in range(BLOCKS):
             triangle(0, r)
+            if r == 0:
+                half_norms(1, 1)
+            if r == 4:
+                h1_parked = park(h_col[1], CHANNELS - 1)
+                fetch(h_row[1], h1_parked)
 
-        project(0, 1, 0)
+        project(0, 0, 0)
         mirror_quarter(0, 0)
-        project(0, 1, 1)
-        mirror_quarter(0, 1)
         quantise_incidence(0, 0, 1)
-        project(0, 1, 2)
+        project(0, 0, 1)
+        mirror_quarter(0, 1)
+        project(0, 0, 2)
         mirror_triangle(0, 0)
-        project(0, 1, 3)
+        project(0, 0, 3)
         mirror_triangle(0, 1)
-        for g in range(HALVES):
-            spread(h_col[1], h_row[1], g)
-        quantise_incidence(0, 1, 0)
-        quantise_xe(0, 1)
-        regroup_incidence(nc.scalar.copy, 0, 0, 0)
+        regroup_incidence(nc.vector.tensor_copy, 0, 0, 0)
+        quantise_xe(0, 0)
         regroup_incidence(nc.scalar.copy, 0, 1, 1)
+        project(0, 1, 0)
+        quantise_incidence(0, 1, 0)
+        sum_degrees(0)
+        project(0, 1, 1)
+        quantise_incidence(0, 0, 0)
+        clamp_degrees(0)
+        project(0, 1, 2)
+        invert_degrees(0)
+        project(0, 1, 3)
+        quantise_incidence(0, 1, 1)
+        quantise_xe(0, 1)
 
         for r in range(PACK):
             upper(1, r, 1)
-            if r == 1:
-                sum_degrees(0)
-            if r == 2:
-                quantise_incidence(0, 0, 0)
-                clamp_degrees(0)
             compare_diagonal(1, 2 * r)
             compare_diagonal(1, 2 * r + 1)
-        regroup_incidence(nc.scalar.copy, 1, 0, 1)
+        edges(0, 0)
+        edges(0, 1)
+        regroup_edges(nc.vector.tensor_copy, 0, 0)
+        regroup_edges(nc.scalar.copy, 0, 1)
         for r in range(BLOCKS):
             triangle(1, r)
             if r == 0:
-                invert_degrees(0)
-                quantise_incidence(0, 1, 1)
+                quantise_edges(0, 0)
+        regroup_incidence(nc.scalar.copy, 1, 0, 1)
         project(1, 0, 0)
         mirror_quarter(1, 0)
+        quantise_edges(0, 1)
         project(1, 0, 1)
         mirror_quarter(1, 1)
-        quantise_incidence(1, 0, 1)
         project(1, 0, 2)
         mirror_triangle(1, 0)
+        quantise_incidence(1, 0, 1)
         project(1, 0, 3)
         mirror_triangle(1, 1)
         quantise_xe(1, 0)
         quantise_incidence(1, 1, 0)
-
-        edges(0, 0)
-        regroup_incidence(nc.vector.tensor_copy, 1, 0, 0)
-        edges(0, 1)
-        regroup_edges(nc.scalar.copy, 0, 1)
-        regroup_edges(nc.vector.tensor_copy, 0, 0)
-        quantise_incidence(1, 0, 0)
-        quantise_edges(0, 0)
-        for ob in range(CHUNKS):
-            if ob == 3:
-                quantise_edges(0, 1)
-            project(1, 1, ob)
-            if ob == 1:
-                sum_degrees(1)
-            if ob == 2:
-                clamp_degrees(1)
-        for g in range(HALVES):
-            spread(r_col[0], r_row[0], g)
+        regroup_incidence(nc.scalar.copy, 1, 0, 0)
         regroup_incidence(nc.scalar.copy, 1, 1, 1)
-        quantise_xe(1, 1)
-        invert_degrees(1)
+        sum_degrees(1)
         for ob in range(CHUNKS):
-            vertices_turned(0, 0, ob)
+            project(1, 1, ob)
+            if ob == 0:
+                clamp_degrees(1)
+            if ob == 1:
+                invert_degrees(1)
             if ob == 2:
+                quantise_incidence(1, 0, 0)
+        quantise_xe(1, 1)
+        for t in range(PACK):
+            vertices(0, 0, t)
+            if t == 0:
                 quantise_incidence(1, 1, 1)
-        edges(1, 0)
-        for ob in range(CHUNKS):
-            add_residual(nc.gpsimd, 0, 0, ob)
-        regroup_edges(nc.vector.tensor_copy, 1, 0)
-        edges(1, 1, (3,))
+        edges_by_word(1, 0, range(CHUNKS))
+        finish(0, 0, 0, 4)
+        edges_by_word(1, 1, range(1))
         quantise_edges(1, 0)
-        regroup_edges(nc.vector.tensor_copy, 1, 1)
-        vertices_turned(0, 1, 0)
+        edges_by_word(1, 1, range(1, CHUNKS))
+        for t in range(PACK):
+            vertices(0, 1, t)
         quantise_edges(1, 1)
-        for ob in range(1, CHUNKS):
-            vertices_turned(0, 1, ob)
         vertices_by_pass(1, 0, (1, 3))
-        for ob in range(CHUNKS):
-            add_residual(nc.gpsimd, 0, 1, ob)
+        finish(0, 1, 0, 4)
         vertices(1, 1, 0)
         vertices(1, 1, 1)
         finish(1, 0, 0, 4)

@@ -19,6 +19,7 @@ THRESHOLD = 16.0
 
 P = 128
 PACK = 4
+PAIR = 2
 K_PASS = P * PACK
 BANK = 512
 
@@ -50,8 +51,8 @@ def half(index):
 
 def tile_hypercomputemodule_pa_kernel(tc, x, W_fc, b_fc, out):
     nc = tc.nc
-    x_dram = x.rearrange("b (cc p) h w -> b p cc (h w)", p=P)
-    out_dram = out.rearrange("b (ob p) h w -> b p ob (h w)", p=P)
+    x_dram = x.rearrange("b (u p e) h w -> b p u e (h w)", p=P, e=PAIR)
+    out_dram = out.rearrange("b (u p e) h w -> b p u e (h w)", p=P, e=PAIR)
 
     with ExitStack() as ctx:
         const = ctx.enter_context(tc.tile_pool(name="const", bufs=1))
@@ -96,12 +97,19 @@ def tile_hypercomputemodule_pa_kernel(tc, x, W_fc, b_fc, out):
         w_sb = const.tile([P, CHUNKS, CHANNELS], BF16)
         w_t = const.tile([P, CHUNKS, CHANNELS], BF16)
         for cc in range(CHUNKS):
-            nc.sync.dma_start(out=x_sb[0][:, cc, half(0)], in_=x_dram[0, :, cc, half(0)])
-        nc.sync.dma_start(out=x_sb[0][:, :, half(1)], in_=x_dram[0, :, :, half(1)])
-        for hf in range(HALVES):
-            nc.sync.dma_start(out=x_sb[1][:, :, half(hf)], in_=x_dram[1, :, :, half(hf)])
-        nc.sync.dma_start(out=w_sb[:], in_=W_fc.rearrange("(ob p) c -> p ob c", p=P))
+            nc.sync.dma_start(out=x_sb[0][:, cc, half(0)], in_=x_dram[0, :, cc // PAIR, cc % PAIR, half(0)])
+        for b, hf in ((0, 1), (1, 0), (1, 1)):
+            for u in range(CHUNKS // PAIR):
+                nc.sync.dma_start(
+                    out=x_sb[b][:, PAIR * u : PAIR * (u + 1), half(hf)], in_=x_dram[b, :, u, :, half(hf)]
+                )
+        nc.sync.dma_start(
+            out=w_sb[:].rearrange("p (u e) c -> p u e c", e=PAIR),
+            in_=W_fc.rearrange("(u p e) c -> p u e c", p=P, e=PAIR),
+        )
         nc.sync.dma_start(out=bias_row[:], in_=b_fc.partition_broadcast(P))
+
+        bias_by_block = bias_row[:].rearrange("p (u o e) -> p u e o", o=P, e=PAIR)
 
         ident_bf = const.tile([P, P], BF16)
         make_identity(nc, ident_bf[:])
@@ -149,11 +157,14 @@ def tile_hypercomputemodule_pa_kernel(tc, x, W_fc, b_fc, out):
                 nc.scalar.copy(out=diag_sb[b][:, PACK * g + t, :], in_=banks[t][:])
 
         def transpose_weights():
-            for cc in range(CHUNKS):
-                bank = psum.tile([P, CHANNELS], BF16, tag="bank")
+            for u in range(CHUNKS // PAIR):
+                bank = psum.tile([P, CHUNKS, P], F32, tag="bank")
                 for ob in range(CHUNKS):
-                    nc.tensor.transpose(bank[:, block(ob)], w_sb[:, ob, block(cc)], ident_bf[:])
-                nc.scalar.copy(out=w_t[:, cc, :], in_=bank[:])
+                    nc.tensor.transpose(bank[:, ob, :], w_sb[:, ob, :].bitcast(F32)[:, block(u)], ident_f32[:])
+                nc.scalar.copy(
+                    out=w_t[:, PAIR * u : PAIR * (u + 1), :],
+                    in_=bank[:].rearrange("p ob o -> p (ob o)").bitcast(BF16).rearrange("p (o e) -> p e o", e=PAIR),
+                )
 
         def half_norms(b, g):
             blocks = slice(PACK * g, PACK * (g + 1))
@@ -314,7 +325,7 @@ def tile_hypercomputemodule_pa_kernel(tc, x, W_fc, b_fc, out):
             nc.vector.tensor_tensor(
                 out=waiting[(b, g)][:, block(ob), :],
                 in0=bank[:].rearrange("p t o -> p o t"),
-                in1=bias_row[:, block(ob)].unsqueeze(2).to_broadcast([P, P, PACK]),
+                in1=bias_by_block[:, ob // PAIR, ob % PAIR, :].unsqueeze(2).to_broadcast([P, P, PACK]),
                 op=ALU.add,
             )
 
@@ -348,32 +359,6 @@ def tile_hypercomputemodule_pa_kernel(tc, x, W_fc, b_fc, out):
                     )
                 scale_rows(t in on_vector, edge_rows[:, t, :], bank[:], b, r)
             waiting[(b, g_out, "edge")] = edge_rows
-
-        def edges_by_word(b, g_out, obs):
-            if 0 in obs:
-                waiting[(b, g_out, "edge grouped")] = stage.tile(
-                    [P, CHANNELS, PACK], BF16, name="edge_grouped", align_bytes=64
-                )
-            for ob in obs:
-                bank = psum.tile([P, PACK, P], F32, tag="bank")
-                for t in range(PACK):
-                    r = PACK * g_out + t
-                    for g in range(PASSES):
-                        nc.tensor.matmul_mx(
-                            out=bank[:, t, :],
-                            lhsT=inc_codes[b][:, g, block(r)].bitcast(FP8X4),
-                            lhsT_scale=inc_scales[b][:, g, block(r)],
-                            rhs=xe_codes[b][:, g, block(ob)].bitcast(FP8X4),
-                            rhs_scale=xe_scales[b][:, g, block(ob)],
-                            start=(g == 0),
-                            stop=(g == PASSES - 1),
-                        )
-                nc.vector.tensor_tensor(
-                    out=waiting[(b, g_out, "edge grouped")][:, block(ob), :],
-                    in0=bank[:].rearrange("p t o -> p o t"),
-                    in1=r_col[b][:, PACK * g_out : PACK * (g_out + 1)].unsqueeze(1).to_broadcast([P, P, PACK]),
-                    op=ALU.mult,
-                )
 
         def regroup_edges(engine_copy, b, g_out):
             edge_grouped = stage.tile([P, CHANNELS, PACK], BF16, name="edge_grouped", align_bytes=64)
@@ -428,11 +413,11 @@ def tile_hypercomputemodule_pa_kernel(tc, x, W_fc, b_fc, out):
                 r = PACK * hf + t
                 scale_rows(t in on_vector, vert[:, t, :], banks[t][:], b, r)
 
-        def finish(b, hf, first, count):
+        def finish(b, hf, first, count, obs=range(CHUNKS)):
             vert = waiting[(b, hf, "vert")]
             width = count * P
             pixels = slice(hf * BANK + first * P, hf * BANK + first * P + width)
-            for ob in range(CHUNKS):
+            for ob in obs:
                 bank = psum.tile([P, PACK, P], F32, tag="bank")
                 for t in range(count):
                     nc.tensor.transpose(bank[:, t, :], vert[:, first + t, block(ob)], ident_f32[:])
@@ -443,7 +428,7 @@ def tile_hypercomputemodule_pa_kernel(tc, x, W_fc, b_fc, out):
                     in1=x_sb[b][:, ob, pixels],
                     op=ALU.add,
                 )
-                nc.sync.dma_start(out=out_dram[b, :, ob, pixels], in_=result[:, :width])
+                nc.sync.dma_start(out=out_dram[b, :, ob // PAIR, ob % PAIR, pixels], in_=result[:, :width])
 
         warm_up()
         gram_diagonal_by_chunk(0, 0)
@@ -532,22 +517,25 @@ def tile_hypercomputemodule_pa_kernel(tc, x, W_fc, b_fc, out):
                 quantise_incidence(1, 0, 0)
         quantise_xe(1, 1)
         for t in range(PACK):
-            vertices(0, 0, t)
+            vertices(0, 0, t, t % 2 == 1)
             if t == 0:
                 quantise_incidence(1, 1, 1)
-        edges_by_word(1, 0, range(CHUNKS))
-        finish(0, 0, 0, 4)
-        edges_by_word(1, 1, range(1))
+        edges(1, 0)
+        edges(1, 1)
+        regroup_edges(nc.vector.tensor_copy, 1, 0)
         quantise_edges(1, 0)
-        edges_by_word(1, 1, range(1, CHUNKS))
+        finish(0, 0, 0, PACK, range(1))
+        regroup_edges(nc.vector.tensor_copy, 1, 1)
+        finish(0, 0, 0, PACK, range(1, 2))
+        quantise_edges(1, 1)
+        finish(0, 0, 0, PACK, range(2, CHUNKS))
         for t in range(PACK):
             vertices(0, 1, t)
-        quantise_edges(1, 1)
         vertices_by_pass(1, 0, (1, 3))
-        finish(0, 1, 0, 4)
+        finish(0, 1, 0, PACK)
         vertices(1, 1, 0)
         vertices(1, 1, 1)
-        finish(1, 0, 0, 4)
+        finish(1, 0, 0, PACK)
         vertices(1, 1, 2)
         vertices(1, 1, 3)
         finish(1, 1, 0, 2)

@@ -36,7 +36,7 @@ PIECES = PIECE_QUARTER + 2
 
 INC_WAITING = 5
 
-WARM_UP = 3
+WARM_UP = 6
 
 FLOPS = BATCH * (2 * PIXELS * PIXELS * CHANNELS * 3 + 2 * PIXELS * CHANNELS * CHANNELS)
 
@@ -68,7 +68,8 @@ def tile_hypercomputemodule_pa_kernel(tc, x, W_fc, b_fc, out):
         sq_col = [keep.tile([P, BLOCKS], F32, name="sq_col%d" % b) for b in batches]
         h_col = [keep.tile([P, P], F32, name="h_col%d" % b) for b in batches]
         h_row = [keep.tile([P, PIXELS], F32, name="h_row%d" % b) for b in batches]
-        r_col = [keep.tile([P, BLOCKS], F32, name="r_col%d" % b) for b in batches]
+        r_row = [keep.tile([P, PIXELS], F32, name="r_row%d" % b) for b in range(1)]
+        r_col = [keep.tile([P, P], F32, name="r_col%d" % b) for b in batches]
         inc = [keep.tile([P, BLOCKS, PIXELS], BF16, name="inc%d" % b) for b in batches]
         degrees = [keep.tile([P, BLOCKS, PIECES], F32, name="degrees%d" % b) for b in batches]
         inc_codes = [
@@ -118,6 +119,7 @@ def tile_hypercomputemodule_pa_kernel(tc, x, W_fc, b_fc, out):
         for b in batches:
             nc.vector.memset(degrees[b][:], 0.0)
         nc.gpsimd.memset(h_col[1][:], 0.0)
+        nc.gpsimd.memset(r_col[0][:], 0.0)
 
         def warm_up():
             for i in range(WARM_UP):
@@ -289,7 +291,7 @@ def tile_hypercomputemodule_pa_kernel(tc, x, W_fc, b_fc, out):
             )
 
         def invert_degrees(b):
-            nc.vector.reciprocal(out=r_col[b][:], in_=waiting[(b, "clamped")][:])
+            nc.vector.reciprocal(out=r_col[b][:, :BLOCKS], in_=waiting[(b, "clamped")][:])
 
         def regroup(engine_copy, grouped, rows):
             engine_copy(
@@ -390,6 +392,29 @@ def tile_hypercomputemodule_pa_kernel(tc, x, W_fc, b_fc, out):
                 )
             scale_rows(on_vector, waiting[(b, hf, "vert")][:, t, :], bank[:], b, r)
 
+        def vertices_turned(b, hf, ob):
+            bank = psum.tile([P, BANK], F32, tag="bank")
+            for g in range(PASSES):
+                nc.tensor.matmul_mx(
+                    out=bank[:],
+                    lhsT=edge_codes[b][:, g, block(ob)].bitcast(FP8X4),
+                    lhsT_scale=edge_scales[b][:, g, block(ob)],
+                    rhs=inc_codes[b][:, g, half(hf)].bitcast(FP8X4),
+                    rhs_scale=inc_scales[b][:, g, half(hf)],
+                    start=(g == 0),
+                    stop=(g == PASSES - 1),
+                )
+            scaled = results.tile([P, BANK], F32, name="scaled", bufs=5)
+            nc.vector.tensor_tensor(out=scaled[:], in0=bank[:], in1=r_row[b][:, half(hf)], op=ALU.mult)
+            waiting[(b, hf, ob, "scaled")] = scaled
+
+        def add_residual(engine, b, hf, ob):
+            result = results.tile([P, BANK], F32, name="result")
+            engine.tensor_tensor(
+                out=result[:], in0=waiting[(b, hf, ob, "scaled")][:], in1=x_sb[b][:, ob, half(hf)], op=ALU.add
+            )
+            nc.sync.dma_start(out=out_dram[b, :, ob // PAIR, ob % PAIR, half(hf)], in_=result[:])
+
         def vertices_by_pass(b, hf, on_vector=()):
             vert = stage.tile([P, PACK, CHANNELS], F32, name="vert", bufs=3)
             waiting[(b, hf, "vert")] = vert
@@ -440,20 +465,19 @@ def tile_hypercomputemodule_pa_kernel(tc, x, W_fc, b_fc, out):
         for g in range(HALVES):
             spread(h_col[0], h_row[0], g)
         half_norms(1, 0)
+        half_norms(1, 1)
 
         for r in range(PACK):
             upper(0, r, 1)
+            if r == 1:
+                h1_parked = park(h_col[1], CHANNELS - 1)
+                fetch(h_row[1], h1_parked)
             compare_diagonal(0, 2 * r)
             compare_diagonal(0, 2 * r + 1)
         transpose_weights()
         regroup_incidence(nc.scalar.copy, 0, 0, 1)
         for r in range(BLOCKS):
             triangle(0, r)
-            if r == 0:
-                half_norms(1, 1)
-            if r == 4:
-                h1_parked = park(h_col[1], CHANNELS - 1)
-                fetch(h_row[1], h1_parked)
 
         project(0, 0, 0)
         mirror_quarter(0, 0)
@@ -485,6 +509,8 @@ def tile_hypercomputemodule_pa_kernel(tc, x, W_fc, b_fc, out):
             compare_diagonal(1, 2 * r + 1)
         edges(0, 0)
         edges(0, 1)
+        r0_parked = park(r_col[0], CHANNELS - 2)
+        fetch(r_row[0], r0_parked)
         regroup_edges(nc.vector.tensor_copy, 0, 0)
         regroup_edges(nc.scalar.copy, 0, 1)
         for r in range(BLOCKS):
@@ -516,22 +542,23 @@ def tile_hypercomputemodule_pa_kernel(tc, x, W_fc, b_fc, out):
             if ob == 2:
                 quantise_incidence(1, 0, 0)
         quantise_xe(1, 1)
-        for t in range(PACK):
-            vertices(0, 0, t, t % 2 == 1)
-            if t == 0:
+        for ob in range(CHUNKS):
+            vertices_turned(0, 0, ob)
+            if ob == 0:
                 quantise_incidence(1, 1, 1)
         edges(1, 0)
         edges(1, 1)
+        for ob in range(2):
+            add_residual(nc.vector, 0, 0, ob)
         regroup_edges(nc.vector.tensor_copy, 1, 0)
         quantise_edges(1, 0)
-        finish(0, 0, 0, PACK, range(1))
         regroup_edges(nc.vector.tensor_copy, 1, 1)
-        finish(0, 0, 0, PACK, range(1, 2))
-        quantise_edges(1, 1)
-        finish(0, 0, 0, PACK, range(2, CHUNKS))
         for t in range(PACK):
             vertices(0, 1, t)
-        vertices_by_pass(1, 0, (1, 3))
+        quantise_edges(1, 1)
+        for ob in range(2, CHUNKS):
+            add_residual(nc.vector, 0, 0, ob)
+        vertices_by_pass(1, 0)
         finish(0, 1, 0, PACK)
         vertices(1, 1, 0)
         vertices(1, 1, 1)

from contextlib import ExitStack

import concourse.mybir as mybir
from concourse.masks import make_identity

F32 = mybir.dt.float32
BF16 = mybir.dt.bfloat16
U32 = mybir.dt.uint32
U8 = mybir.dt.uint8
FP8X4 = mybir.dt.float8_e4m3fn_x4
ALU = mybir.AluOpType
ACT = mybir.ActivationFunctionType
AXIS = mybir.AxisListType

BATCH = 2
CHANNELS = 512
PIXELS = 1024
THRESHOLD = 16.0

P = 128
PACK = 4
PAIR = 2
K_PASS = P * PACK
BANK = 512

CHUNKS = CHANNELS // P
BLOCKS = PIXELS // P
PASSES = PIXELS // K_PASS
HALVES = PIXELS // BANK

PIECE_DIAGONAL = 0
PIECE_UPPER = 1
PIECE_LOWER = PIECE_UPPER + HALVES
PIECE_QUARTER = PIECE_LOWER + 1
PIECES = PIECE_QUARTER + 2

INC_WAITING = 5

WARM_UP = 6

FLOPS = BATCH * (2 * PIXELS * PIXELS * CHANNELS * 3 + 2 * PIXELS * CHANNELS * CHANNELS)


def block(index):
    return slice(index * P, (index + 1) * P)


def half(index):
    return slice(index * BANK, (index + 1) * BANK)


def tile_hypercomputemodule_pa_kernel(tc, x, W_fc, b_fc, out):
    nc = tc.nc
    x_dram = x.rearrange("b (u p e) h w -> b p u e (h w)", p=P, e=PAIR)
    out_dram = out.rearrange("b (u p e) h w -> b p u e (h w)", p=P, e=PAIR)

    with ExitStack() as ctx:
        const = ctx.enter_context(tc.tile_pool(name="const", bufs=1))
        keep = ctx.enter_context(tc.tile_pool(name="keep", bufs=1))
        stage = ctx.enter_context(tc.tile_pool(name="stage", bufs=2))
        results = ctx.enter_context(tc.tile_pool(name="results", bufs=8))
        psum = ctx.enter_context(tc.psum_pool(name="psum", bufs=8))
        ctx.enter_context(tc.manual_schedule())

        batches = range(BATCH)
        x_sb = [keep.tile([P, CHUNKS, PIXELS], BF16, name="x_sb%d" % b) for b in batches]
        diag_sb = [keep.tile([P, BLOCKS, P], F32, name="diag_sb%d" % b) for b in batches]
        sq_col = [keep.tile([P, BLOCKS], F32, name="sq_col%d" % b) for b in batches]
        h_col = [keep.tile([P, P], F32, name="h_col%d" % b) for b in batches]
        h_row = [keep.tile([P, PIXELS], F32, name="h_row%d" % b) for b in batches]
        r_row = [keep.tile([P, PIXELS], F32, name="r_row%d" % b) for b in range(1)]
        r_col = [keep.tile([P, P], F32, name="r_col%d" % b) for b in batches]
        inc = [keep.tile([P, BLOCKS, PIXELS], BF16, name="inc%d" % b) for b in batches]
        degrees = [keep.tile([P, BLOCKS, PIECES], F32, name="degrees%d" % b) for b in batches]
        inc_codes = [
            keep.tile([P, PASSES, PIXELS], U32, name="inc_codes%d" % b, align_bytes=64) for b in batches
        ]
        inc_scales = [
            keep.tile([P, PASSES, PIXELS], U8, name="inc_scales%d" % b, align_bytes=64) for b in batches
        ]
        xe_codes = [
            keep.tile([P, PASSES, CHANNELS], U32, name="xe_codes%d" % b, align_bytes=64) for b in batches
        ]
        xe_scales = [
            keep.tile([P, PASSES, CHANNELS], U8, name="xe_scales%d" % b, align_bytes=64) for b in batches
        ]
        edge_codes = [
            keep.tile([P, PASSES, CHANNELS], U32, name="edge_codes%d" % b, align_bytes=64) for b in batches
        ]
        edge_scales = [
            keep.tile([P, PASSES, CHANNELS], U8, name="edge_scales%d" % b, align_bytes=64) for b in batches
        ]
        waiting = {}

        warm = const.tile([P, BANK], BF16)
        nc.vector.memset(warm[:], 0.0)
        bias_row = const.tile([P, CHANNELS], BF16)
        w_sb = const.tile([P, CHUNKS, CHANNELS], BF16)
        w_t = const.tile([P, CHUNKS, CHANNELS], BF16)
        for cc in range(CHUNKS):
            nc.sync.dma_start(out=x_sb[0][:, cc, half(0)], in_=x_dram[0, :, cc // PAIR, cc % PAIR, half(0)])
        for b, hf in ((0, 1), (1, 0), (1, 1)):
            for u in range(CHUNKS // PAIR):
                nc.sync.dma_start(
                    out=x_sb[b][:, PAIR * u : PAIR * (u + 1), half(hf)], in_=x_dram[b, :, u, :, half(hf)]
                )
        nc.sync.dma_start(
            out=w_sb[:].rearrange("p (u e) c -> p u e c", e=PAIR),
            in_=W_fc.rearrange("(u p e) c -> p u e c", p=P, e=PAIR),
        )
        nc.sync.dma_start(out=bias_row[:], in_=b_fc.partition_broadcast(P))

        bias_by_block = bias_row[:].rearrange("p (u o e) -> p u e o", o=P, e=PAIR)

        ident_bf = const.tile([P, P], BF16)
        make_identity(nc, ident_bf[:])
        ident_f32 = const.tile([P, P], F32)
        make_identity(nc, ident_f32[:])
        for b in batches:
            nc.vector.memset(degrees[b][:], 0.0)
        nc.gpsimd.memset(h_col[1][:], 0.0)
        nc.gpsimd.memset(r_col[0][:], 0.0)

        def warm_up():
            for i in range(WARM_UP):
                bank = psum.tile([P, BANK], F32, tag="bank")
                nc.tensor.matmul(out=bank[:], lhsT=warm[:, block(0)], rhs=warm[:], start=True, stop=True)

        def gram_diagonal(b, g):
            bank = psum.tile([P, PACK, P], F32, tag="bank")
            for t in range(PACK):
                rows = block(PACK * g + t)
                for cc in range(CHUNKS):
                    nc.tensor.matmul(
                        out=bank[:, t, :],
                        lhsT=x_sb[b][:, cc, rows],
                        rhs=x_sb[b][:, cc, rows],
                        start=(cc == 0),
                        stop=(cc == CHUNKS - 1),
                    )
            nc.scalar.copy(out=diag_sb[b][:, PACK * g : PACK * (g + 1), :], in_=bank[:])

        def gram_diagonal_by_chunk(b, g):
            banks = []
            for cc in range(CHUNKS):
                for t in range(PACK):
                    rows = block(PACK * g + t)
                    if cc == 0:
                        bank = psum.tile([P, P], F32, tag="bank")
                        banks.append(bank)
                    nc.tensor.matmul(
                        out=banks[t][:],
                        lhsT=x_sb[b][:, cc, rows],
                        rhs=x_sb[b][:, cc, rows],
                        start=(cc == 0),
                        stop=(cc == CHUNKS - 1),
                    )
            for t in range(PACK):
                nc.scalar.copy(out=diag_sb[b][:, PACK * g + t, :], in_=banks[t][:])

        def transpose_weights():
            for u in range(CHUNKS // PAIR):
                bank = psum.tile([P, CHUNKS, P], F32, tag="bank")
                for ob in range(CHUNKS):
                    nc.tensor.transpose(bank[:, ob, :], w_sb[:, ob, :].bitcast(F32)[:, block(u)], ident_f32[:])
                nc.scalar.copy(
                    out=w_t[:, PAIR * u : PAIR * (u + 1), :],
                    in_=bank[:].rearrange("p ob o -> p (ob o)").bitcast(BF16).rearrange("p (o e) -> p e o", e=PAIR),
                )

        def half_norms(b, g):
            blocks = slice(PACK * g, PACK * (g + 1))
            masked = stage.tile([P, PACK, P], F32)
            for t in range(PACK):
                r = PACK * g + t
                nc.vector.scalar_tensor_tensor(
                    out=masked[:, t, :],
                    in0=diag_sb[b][:, r, :],
                    scalar=1.0,
                    in1=ident_f32[:],
                    op0=ALU.mult,
                    op1=ALU.mult,
                    accum_out=sq_col[b][:, r : r + 1],
                )
            nc.vector.tensor_scalar(
                out=h_col[b][:, blocks],
                in0=sq_col[b][:, blocks],
                scalar1=0.5,
                scalar2=-THRESHOLD * THRESHOLD / 4.0,
                op0=ALU.mult,
                op1=ALU.add,
            )

        def spread(col, row, g):
            bank = psum.tile([P, PACK, P], F32, tag="bank")
            for t in range(PACK):
                r = PACK * g + t
                nc.tensor.transpose(bank[:, t, :], col[:, r : r + 1].to_broadcast([P, P]), ident_f32[:])
            nc.scalar.copy(out=row[:, half(g)], in_=bank[:].rearrange("p t n -> p (t n)"))

        def park(col, channel):
            bank = psum.tile([P, P], F32, tag="bank")
            nc.tensor.transpose(bank[:], col[:], ident_f32[:])
            line = stage.tile([BLOCKS, P], F32)
            nc.scalar.copy(out=line[:], in_=bank[:BLOCKS, :])
            parked = out[BATCH - 1, channel].rearrange("h w -> (h w)")
            nc.sync.dma_start(out=parked.rearrange("(r p) -> r p", p=P), in_=line[:])
            return parked

        def fetch(row, parked):
            nc.sync.dma_start(out=row[:], in_=parked.partition_broadcast(P))

        def compare(b, r, gram, cols, piece):
            nc.vector.scalar_tensor_tensor(
                out=inc[b][:, r, cols],
                in0=gram,
                scalar=h_col[b][:, r : r + 1],
                in1=h_row[b][:, cols],
                op0=ALU.subtract,
                op1=ALU.is_gt,
                accum_out=degrees[b][:, r, piece : piece + 1],
            )

        def upper(b, r, hf):
            first = max(hf * BANK, (r + 1) * P)
            width = (hf + 1) * BANK - first
            cols = slice(first, first + width)
            bank = psum.tile([P, BANK], F32, tag="bank")
            for cc in range(CHUNKS):
                nc.tensor.matmul(
                    out=bank[:, :width],
                    lhsT=x_sb[b][:, cc, block(r)],
                    rhs=x_sb[b][:, cc, cols],
                    start=(cc == 0),
                    stop=(cc == CHUNKS - 1),
                )
            compare(b, r, bank[:, :width], cols, PIECE_UPPER + hf)

        def compare_diagonal(b, r):
            compare(b, r, diag_sb[b][:, r, :], block(r), PIECE_DIAGONAL)

        def triangle(b, r):
            if r % PACK < PACK - 1:
                upper(b, r, r // PACK)

        def mirror_triangle(b, g):
            for r in range(PACK * g + 1, PACK * (g + 1)):
                first = PACK * g
                width = (r - first) * P
                bank = psum.tile([P, BANK], BF16, tag="bank")
                for q in range(first, r):
                    nc.tensor.transpose(bank[:, block(q - first)], inc[b][:, q, block(r)], ident_bf[:])
                nc.scalar.activation(
                    out=inc[b][:, r, first * P : first * P + width],
                    in_=bank[:, :width],
                    func=ACT.Copy,
                    accum_out=degrees[b][:, r, PIECE_LOWER : PIECE_LOWER + 1],
                )

        def mirror_quarter(b, pair):
            if pair == 0:
                waiting[(b, 1, 0)] = stage.tile(
                    [P, BANK, PACK], BF16, name="inc_grouped", align_bytes=64, bufs=INC_WAITING
                )
            grouped = waiting[(b, 1, 0)]
            bank = psum.tile([P, 2, PACK, P], BF16, tag="bank")
            for i in range(2):
                q = 2 * pair + i
                for t in range(PACK):
                    nc.tensor.transpose(bank[:, i, t, :], inc[b][:, q, block(PACK + t)], ident_bf[:])
            nc.scalar.copy(
                out=grouped[:, 2 * P * pair : 2 * P * (pair + 1), :].rearrange("p (q c) t -> p q c t", q=2),
                in_=bank[:].rearrange("p q t c -> p q c t"),
            )
            nc.vector.tensor_reduce(
                out=degrees[b][:, PACK : 2 * PACK, PIECE_QUARTER + pair],
                in_=bank[:].rearrange("p q t c -> p t q c"),
                axis=AXIS.XY,
                op=ALU.add,
            )
        def sum_degrees(b):
            waiting[(b, "degree")] = stage.tile([P, BLOCKS], F32, name="degree")
            nc.vector.tensor_reduce(
                out=waiting[(b, "degree")][:], in_=degrees[b][:], axis=AXIS.X, op=ALU.add
            )

        def clamp_degrees(b):
            waiting[(b, "clamped")] = stage.tile([P, BLOCKS], F32, name="clamped")
            nc.vector.tensor_scalar_max(
                out=waiting[(b, "clamped")][:], in0=waiting[(b, "degree")][:], scalar1=1.0
            )

        def invert_degrees(b):
            nc.vector.reciprocal(out=r_col[b][:, :BLOCKS], in_=waiting[(b, "clamped")][:])

        def regroup(engine_copy, grouped, rows):
            engine_copy(
                out=grouped.rearrange("p (c i) t -> p c t i", i=4),
                in_=rows.rearrange("p t (c i) -> p c t i", i=4),
            )

        def regroup_incidence(engine_copy, b, g, hf):
            grouped = stage.tile([P, BANK, PACK], BF16, name="inc_grouped", align_bytes=64, bufs=INC_WAITING)
            regroup(engine_copy, grouped[:], inc[b][:, PACK * g : PACK * (g + 1), half(hf)])
            waiting[(b, g, hf)] = grouped

        def quantise_incidence(b, g, hf):
            nc.vector.quantize_mx(
                out=inc_codes[b][:, g, half(hf)].bitcast(FP8X4),
                scales=inc_scales[b][:, g, half(hf)],
                in_=waiting[(b, g, hf)][:].rearrange("p c t -> p (c t)"),
            )

        def project(b, g, ob):
            if ob == 0:
                waiting[(b, g)] = stage.tile([P, CHANNELS, PACK], BF16, name="xe_grouped", align_bytes=64)
            bank = psum.tile([P, PACK, P], F32, tag="bank")
            for t in range(PACK):
                for cc in range(CHUNKS):
                    nc.tensor.matmul(
                        out=bank[:, t, :],
                        lhsT=x_sb[b][:, cc, block(PACK * g + t)],
                        rhs=w_t[:, cc, block(ob)],
                        start=(cc == 0),
                        stop=(cc == CHUNKS - 1),
                    )
            nc.vector.tensor_tensor(
                out=waiting[(b, g)][:, block(ob), :],
                in0=bank[:].rearrange("p t o -> p o t"),
                in1=bias_by_block[:, ob // PAIR, ob % PAIR, :].unsqueeze(2).to_broadcast([P, P, PACK]),
                op=ALU.add,
            )

        def quantise_xe(b, g):
            nc.vector.quantize_mx(
                out=xe_codes[b][:, g, :].bitcast(FP8X4),
                scales=xe_scales[b][:, g, :],
                in_=waiting[(b, g)][:].rearrange("p o t -> p (o t)"),
            )

        def scale_rows(on_vector, out, sums, b, r):
            if on_vector:
                nc.vector.tensor_scalar_mul(out=out, in0=sums, scalar1=r_col[b][:, r : r + 1])
            else:
                nc.scalar.activation(out=out, in_=sums, func=ACT.Copy, scale=r_col[b][:, r : r + 1])

        def edges(b, g_out, on_vector=()):
            edge_rows = stage.tile([P, PACK, CHANNELS], BF16)
            for t in range(PACK):
                r = PACK * g_out + t
                bank = psum.tile([P, CHANNELS], F32, tag="bank")
                for g in range(PASSES):
                    nc.tensor.matmul_mx(
                        out=bank[:],
                        lhsT=inc_codes[b][:, g, block(r)].bitcast(FP8X4),
                        lhsT_scale=inc_scales[b][:, g, block(r)],
                        rhs=xe_codes[b][:, g, :].bitcast(FP8X4),
                        rhs_scale=xe_scales[b][:, g, :],
                        start=(g == 0),
                        stop=(g == PASSES - 1),
                    )
                scale_rows(t in on_vector, edge_rows[:, t, :], bank[:], b, r)
            waiting[(b, g_out, "edge")] = edge_rows

        def regroup_edges(engine_copy, b, g_out):
            edge_grouped = stage.tile([P, CHANNELS, PACK], BF16, name="edge_grouped", align_bytes=64)
            regroup(engine_copy, edge_grouped[:], waiting[(b, g_out, "edge")][:])
            waiting[(b, g_out, "edge grouped")] = edge_grouped

        def quantise_edges(b, g_out):
            edge_grouped = waiting[(b, g_out, "edge grouped")]
            nc.vector.quantize_mx(
                out=edge_codes[b][:, g_out, :].bitcast(FP8X4),
                scales=edge_scales[b][:, g_out, :],
                in_=edge_grouped[:].rearrange("p o t -> p (o t)"),
            )

        def vertices(b, hf, t, on_vector=False):
            if t == 0:
                waiting[(b, hf, "vert")] = stage.tile([P, PACK, CHANNELS], F32, name="vert", bufs=3)
            r = PACK * hf + t
            bank = psum.tile([P, CHANNELS], F32, tag="bank")
            for g in range(PASSES):
                nc.tensor.matmul_mx(
                    out=bank[:],
                    lhsT=inc_codes[b][:, g, block(r)].bitcast(FP8X4),
                    lhsT_scale=inc_scales[b][:, g, block(r)],
                    rhs=edge_codes[b][:, g, :].bitcast(FP8X4),
                    rhs_scale=edge_scales[b][:, g, :],
                    start=(g == 0),
                    stop=(g == PASSES - 1),
                )
            scale_rows(on_vector, waiting[(b, hf, "vert")][:, t, :], bank[:], b, r)

        def vertices_turned(b, hf, ob):
            bank = psum.tile([P, BANK], F32, tag="bank")
            for g in range(PASSES):
                nc.tensor.matmul_mx(
                    out=bank[:],
                    lhsT=edge_codes[b][:, g, block(ob)].bitcast(FP8X4),
                    lhsT_scale=edge_scales[b][:, g, block(ob)],
                    rhs=inc_codes[b][:, g, half(hf)].bitcast(FP8X4),
                    rhs_scale=inc_scales[b][:, g, half(hf)],
                    start=(g == 0),
                    stop=(g == PASSES - 1),
                )
            scaled = results.tile([P, BANK], F32, name="scaled", bufs=5)
            nc.vector.tensor_tensor(out=scaled[:], in0=bank[:], in1=r_row[b][:, half(hf)], op=ALU.mult)
            waiting[(b, hf, ob, "scaled")] = scaled

        def add_residual(engine, b, hf, ob):
            result = results.tile([P, BANK], F32, name="result")
            engine.tensor_tensor(
                out=result[:], in0=waiting[(b, hf, ob, "scaled")][:], in1=x_sb[b][:, ob, half(hf)], op=ALU.add
            )
            nc.sync.dma_start(out=out_dram[b, :, ob // PAIR, ob % PAIR, half(hf)], in_=result[:])

        def vertices_by_pass(b, hf, on_vector=()):
            vert = stage.tile([P, PACK, CHANNELS], F32, name="vert", bufs=3)
            waiting[(b, hf, "vert")] = vert
            banks = []
            for g in range(PASSES):
                for t in range(PACK):
                    r = PACK * hf + t
                    if g == 0:
                        bank = psum.tile([P, CHANNELS], F32, tag="bank")
                        banks.append(bank)
                    nc.tensor.matmul_mx(
                        out=banks[t][:],
                        lhsT=inc_codes[b][:, g, block(r)].bitcast(FP8X4),
                        lhsT_scale=inc_scales[b][:, g, block(r)],
                        rhs=edge_codes[b][:, g, :].bitcast(FP8X4),
                        rhs_scale=edge_scales[b][:, g, :],
                        start=(g == 0),
                        stop=(g == PASSES - 1),
                    )
            for t in range(PACK):
                r = PACK * hf + t
                scale_rows(t in on_vector, vert[:, t, :], banks[t][:], b, r)

        def finish(b, hf, first, count, obs=range(CHUNKS)):
            vert = waiting[(b, hf, "vert")]
            width = count * P
            pixels = slice(hf * BANK + first * P, hf * BANK + first * P + width)
            for ob in obs:
                bank = psum.tile([P, PACK, P], F32, tag="bank")
                for t in range(count):
                    nc.tensor.transpose(bank[:, t, :], vert[:, first + t, block(ob)], ident_f32[:])
                result = results.tile([P, BANK], F32, name="result")
                nc.vector.tensor_tensor(
                    out=result[:, :width],
                    in0=bank[:, :count, :].rearrange("p t i -> p (t i)"),
                    in1=x_sb[b][:, ob, pixels],
                    op=ALU.add,
                )
                nc.sync.dma_start(out=out_dram[b, :, ob // PAIR, ob % PAIR, pixels], in_=result[:, :width])

        warm_up()
        gram_diagonal_by_chunk(0, 0)
        gram_diagonal(0, 1)
        half_norms(0, 0)
        gram_diagonal(1, 0)
        half_norms(0, 1)
        gram_diagonal(1, 1)
        for g in range(HALVES):
            spread(h_col[0], h_row[0], g)
        half_norms(1, 0)
        half_norms(1, 1)

        for r in range(PACK):
            upper(0, r, 1)
            if r == 1:
                h1_parked = park(h_col[1], CHANNELS - 1)
                fetch(h_row[1], h1_parked)
            compare_diagonal(0, 2 * r)
            compare_diagonal(0, 2 * r + 1)
        transpose_weights()
        regroup_incidence(nc.scalar.copy, 0, 0, 1)
        for r in range(BLOCKS):
            triangle(0, r)

        project(0, 0, 0)
        mirror_quarter(0, 0)
        quantise_incidence(0, 0, 1)
        project(0, 0, 1)
        mirror_quarter(0, 1)
        project(0, 0, 2)
        mirror_triangle(0, 0)
        project(0, 0, 3)
        mirror_triangle(0, 1)
        regroup_incidence(nc.vector.tensor_copy, 0, 0, 0)
        quantise_xe(0, 0)
        regroup_incidence(nc.scalar.copy, 0, 1, 1)
        project(0, 1, 0)
        quantise_incidence(0, 1, 0)
        sum_degrees(0)
        project(0, 1, 1)
        quantise_incidence(0, 0, 0)
        clamp_degrees(0)
        project(0, 1, 2)
        invert_degrees(0)
        project(0, 1, 3)
        quantise_incidence(0, 1, 1)
        quantise_xe(0, 1)

        for r in range(PACK):
            upper(1, r, 1)
            compare_diagonal(1, 2 * r)
            compare_diagonal(1, 2 * r + 1)
        edges(0, 0)
        edges(0, 1)
        r0_parked = park(r_col[0], CHANNELS - 2)
        fetch(r_row[0], r0_parked)
        regroup_edges(nc.vector.tensor_copy, 0, 0)
        regroup_edges(nc.scalar.copy, 0, 1)
        for r in range(BLOCKS):
            triangle(1, r)
            if r == 0:
                quantise_edges(0, 0)
        regroup_incidence(nc.scalar.copy, 1, 0, 1)
        project(1, 0, 0)
        mirror_quarter(1, 0)
        quantise_edges(0, 1)
        project(1, 0, 1)
        mirror_quarter(1, 1)
        project(1, 0, 2)
        mirror_triangle(1, 0)
        quantise_incidence(1, 0, 1)
        project(1, 0, 3)
        mirror_triangle(1, 1)
        quantise_xe(1, 0)
        quantise_incidence(1, 1, 0)
        regroup_incidence(nc.scalar.copy, 1, 0, 0)
        regroup_incidence(nc.scalar.copy, 1, 1, 1)
        sum_degrees(1)
        for ob in range(CHUNKS):
            project(1, 1, ob)
            if ob == 0:
                clamp_degrees(1)
            if ob == 1:
                invert_degrees(1)
            if ob == 2:
                quantise_incidence(1, 0, 0)
        quantise_xe(1, 1)
        for ob in range(CHUNKS):
            vertices_turned(0, 0, ob)
            if ob == 0:
                quantise_incidence(1, 1, 1)
        edges(1, 0)
        edges(1, 1)
        for ob in range(2):
            add_residual(nc.vector, 0, 0, ob)
        regroup_edges(nc.vector.tensor_copy, 1, 0)
        quantise_edges(1, 0)
        regroup_edges(nc.vector.tensor_copy, 1, 1)
        for t in range(PACK):
            vertices(0, 1, t)
        quantise_edges(1, 1)
        for ob in range(2, CHUNKS):
            add_residual(nc.vector, 0, 0, ob)
        vertices_by_pass(1, 0)
        finish(0, 1, 0, PACK)
        vertices(1, 1, 0)
        vertices(1, 1, 1)
        finish(1, 0, 0, PACK)
        vertices(1, 1, 2)
        vertices(1, 1, 3)
        finish(1, 1, 0, 2)
        finish(1, 1, 2, 2)
